import numpy as np
import ml_dtypes


def mxq(x, axis, fmt="e4m3"):
    dtype, down = {"e4m3": (ml_dtypes.float8_e4m3fn, 7), "e5m2": (ml_dtypes.float8_e5m2, 14)}[fmt]
    v = np.moveaxis(np.asarray(x, np.float32).astype(ml_dtypes.bfloat16).astype(np.float64), axis, -1)
    blocks = v.reshape(v.shape[:-1] + (-1, 32))
    amax = np.abs(blocks).max(-1, keepdims=True)
    byte = np.maximum(np.where(amax > 0, np.frexp(amax)[1] - 1 + 127, 0) - down, 1)
    scale = np.exp2(byte - 127.0)
    codes = (blocks / scale).astype(np.float32).astype(dtype).astype(np.float64)
    return np.moveaxis((codes * scale).reshape(v.shape), -1, axis)


WIDE = False


def mx_kscale(k):
    if not WIDE:
        return np.ones(k)
    levels = np.array([10, -10, 5, -5, 0])
    a = np.random.permutation(np.resize(levels, k // 512 * 4)).reshape(k // 512, 4)
    idx = np.arange(k)
    return np.exp2(a[idx // 512, idx % 128 // 32])


BF16 = ml_dtypes.bfloat16


def bf(x):
    return np.asarray(x, np.float32).astype(BF16)


def f64(x):
    return np.asarray(x).astype(np.float64)


E2M1 = np.array([0.0, 0.5, 1.0, 1.5, 2.0, 3.0, 4.0, 6.0, -0.0, -0.5, -1.0, -1.5, -2.0, -3.0, -4.0, -6.0])


def pack_weight(w, fmt):
    k, n = w.shape
    w = f64(bf(w)).reshape(k // 32, 32, n)
    amax = np.abs(w).max(1)
    if fmt == "e4m3":
        byte = np.frexp(amax)[1] - 1 + 127 - 7
    else:
        mant, ex = np.frexp(amax / 6.0)
        byte = np.where(mant > 0.5, ex, ex - 1) + 127
    byte = np.clip(np.where(amax > 0, byte, 1), 1, 254)
    scaled = (w * np.exp2(127.0 - byte)[:, None, :]).reshape(k, n).astype(np.float32)
    by_word = np.ascontiguousarray(scaled.reshape(k // 512, 128, 4, n).transpose(0, 1, 3, 2))
    if fmt == "e4m3":
        words = by_word.astype(ml_dtypes.float8_e4m3fn).view(np.uint8)
    else:
        c = by_word.astype(ml_dtypes.float4_e2m1fn).view(np.uint8) & 0xF
        words = c[..., 0::2] | (c[..., 1::2] << 4)
    return np.ascontiguousarray(words), np.ascontiguousarray(byte.astype(np.uint8).reshape(k // 512, 16, n))


def unpack_weight(words, scales, fmt):
    g, p, n, _ = words.shape
    if fmt == "e4m3":
        vals = np.ascontiguousarray(words).view(ml_dtypes.float8_e4m3fn).astype(np.float64)
    else:
        nib = np.empty((g, p, n, 4), np.uint8)
        nib[..., 0::2] = words & 0xF
        nib[..., 1::2] = words >> 4
        vals = E2M1[nib]
    vals = vals * np.repeat(np.exp2(scales.astype(np.float64) - 127.0), 8, axis=1)[..., None]
    return vals.transpose(0, 1, 3, 2).reshape(g * 512, n)

def pack4(w):
    words, scales = pack_weight(w, "e2m1")
    return words.reshape(words.shape[0], 128, -1), scales


def unpack4(words, scales):
    return unpack_weight(words.reshape(words.shape[0], 128, -1, 2), scales, "e2m1")


B, L_IMG, L_TXT, DM, H, D = 1, 6144, 2048, 512, 2, 64
L = L_TXT + L_IMG
HD = H * D
EPS = 1e-6


def rms(x, gain):
    return x / np.sqrt(np.mean(np.square(x), axis=-1, keepdims=True) + EPS) * gain


def qkv(x, w, qn, kn):
    y = (mxq(x, 2, "e4m3") @ w).reshape(x.shape[0], x.shape[1], 3, H, D)
    return rms(y[:, :, 0], qn), rms(y[:, :, 1], kn), y[:, :, 2]


def rope(x, fc):
    x_ = x.reshape(x.shape[:-1] + (D // 2, 1, 2))
    out = fc[:, None, :, :, 0] * x_[..., 0] + fc[:, None, :, :, 1] * x_[..., 1]
    return out.reshape(x.shape)


def setup_inputs():
    s = mx_kscale(DM)
    r = np.random.standard_normal
    hidden_states = bf(r((B, L_IMG, DM)) * s)
    encoder_hidden_states = bf(r((B, L_TXT, DM)) * s)
    image_rotary_emb = bf(r((L, D // 2, 4)) * 0.6)
    iqkv_words, iqkv_scales = pack4(r((DM, 3 * HD)) / np.sqrt(DM) / s[:, None])
    eqkv_words, eqkv_scales = pack4(r((DM, 3 * HD)) / np.sqrt(DM) / s[:, None])
    return {
        "hidden_states": hidden_states,
        "encoder_hidden_states": encoder_hidden_states,
        "image_rotary_emb": image_rotary_emb,
        "W_iqkv_words": iqkv_words,
        "W_iqkv_scales": iqkv_scales,
        "W_eqkv_words": eqkv_words,
        "W_eqkv_scales": eqkv_scales,
        "qn_scale": bf(1.0 + 0.1 * r(D)),
        "kn_scale": bf(1.0 + 0.1 * r(D)),
        "eqn_scale": bf(1.0 + 0.1 * r(D)),
        "ekn_scale": bf(1.0 + 0.1 * r(D)),
    }


def reference(hidden_states, encoder_hidden_states, image_rotary_emb, W_iqkv_words, W_iqkv_scales, W_eqkv_words, W_eqkv_scales, qn_scale, kn_scale, eqn_scale, ekn_scale):
    q, k, v = qkv(f64(hidden_states), unpack4(W_iqkv_words, W_iqkv_scales), f64(qn_scale), f64(kn_scale))
    eq, ek, ev = qkv(f64(encoder_hidden_states), unpack4(W_eqkv_words, W_eqkv_scales), f64(eqn_scale), f64(ekn_scale))
    q = np.concatenate((eq, q), axis=1)
    k = np.concatenate((ek, k), axis=1)
    v = np.concatenate((ev, v), axis=1)
    fc = f64(image_rotary_emb).reshape(L, D // 2, 2, 2)
    return rope(q, fc).reshape(B, L, HD), rope(k, fc).reshape(B, L, HD), v.reshape(B, L, HD)

@@ -1,0 +1,261 @@
+from contextlib import ExitStack
+
+import concourse.mybir as mybir
+from concourse.masks import make_identity
+
+F32 = mybir.dt.float32
+BF16 = mybir.dt.bfloat16
+I32 = mybir.dt.int32
+U32 = mybir.dt.uint32
+U8 = mybir.dt.uint8
+FP8X4 = mybir.dt.float8_e4m3fn_x4
+FP4X4 = mybir.dt.float4_e2m1fn_x4
+ACT = mybir.ActivationFunctionType
+ALU = mybir.AluOpType
+
+P = 128
+DM = 512
+L_TXT = 2048
+L_IMG = 6144
+HEADS = 2
+D = 64
+HD = HEADS * D
+N_QK = 2 * HD
+N_QKV = 3 * HD
+EPS = 1e-6
+
+T = 8
+CHUNK = P * T
+N_CHUNKS = (L_TXT + L_IMG) // CHUNK
+TXT_CHUNKS = L_TXT // CHUNK
+GT = 4
+GROUPS_PER_CHUNK = T // GT
+N_GROUPS = N_CHUNKS * GROUPS_PER_CHUNK
+NORMS = 2 * HEADS
+
+FLOPS = 2 * (L_TXT + L_IMG) * DM * N_QKV
+
+
+def load_weight(nc, consts, words_dram, scales_dram, label):
+    words = consts.tile([P, 2 * N_QKV], U8, name=label + "_words", align_bytes=64)
+    nc.sync.dma_start(out=words[:].bitcast(I32), in_=words_dram[0].bitcast(I32))
+    plane = consts.tile([P, N_QKV], U8, name=label + "_plane", align_bytes=64)
+    nc.vector.memset(plane[:].bitcast(I32), 0)
+    for quadrant in range(4):
+        nc.sync.dma_start(
+            out=plane[32 * quadrant : 32 * quadrant + 4, :].bitcast(I32),
+            in_=scales_dram[0, 4 * quadrant : 4 * quadrant + 4, :].bitcast(I32),
+        )
+    return words, plane
+
+
+def load_gains(nc, consts, q_gain, k_gain, label):
+    raw = consts.tile([P, 2, D], BF16, name=label + "_gain")
+    nc.scalar.dma_start(out=raw[:, 0, :], in_=q_gain.partition_broadcast(P))
+    nc.scalar.dma_start(out=raw[:, 1, :], in_=k_gain.partition_broadcast(P))
+    spread = consts.tile([P, 2, 2 * D], BF16, name=label + "_gain_spread")
+    for qk in range(2):
+        nc.vector.tensor_copy(
+            out=spread[:, qk, :].rearrange("p (i a b) -> p i a b", a=2, b=2),
+            in_=raw[:, qk, :].rearrange("p (i o b) -> p i o b", o=1, b=2).to_broadcast([P, D // 2, 2, 2]),
+        )
+    return spread
+
+
+def tile_fluxattention_pa_t_kernel(
+    tc,
+    hidden_states,
+    encoder_hidden_states,
+    image_rotary_emb,
+    W_iqkv_words,
+    W_iqkv_scales,
+    W_eqkv_words,
+    W_eqkv_scales,
+    qn_scale,
+    kn_scale,
+    eqn_scale,
+    ekn_scale,
+    out_0,
+    out_1,
+    out_2,
+):
+    nc = tc.nc
+    with ExitStack() as ctx:
+        consts = ctx.enter_context(tc.tile_pool(name="consts", bufs=1))
+        x_pool = ctx.enter_context(tc.tile_pool(name="x", bufs=N_GROUPS))
+        table_pool = ctx.enter_context(tc.tile_pool(name="table", bufs=N_CHUNKS))
+        work = ctx.enter_context(tc.tile_pool(name="work", bufs=2))
+        deep = ctx.enter_context(tc.tile_pool(name="deep", bufs=3))
+        xt_psum = ctx.enter_context(tc.psum_pool(name="xt_psum", bufs=2))
+        qk_psum = ctx.enter_context(tc.psum_pool(name="qk_psum", bufs=4))
+        v_psum = ctx.enter_context(tc.psum_pool(name="v_psum", bufs=2))
+        ctx.enter_context(tc.manual_schedule())
+
+        def chunk_rows(c):
+            if c < TXT_CHUNKS:
+                rows = encoder_hidden_states[0, c * CHUNK : (c + 1) * CHUNK, :]
+            else:
+                rows = hidden_states[0, (c - TXT_CHUNKS) * CHUNK : (c - TXT_CHUNKS + 1) * CHUNK, :]
+            return rows.rearrange("(p t) k -> p t k", t=T)
+
+        x_tiles = []
+        table_tiles = []
+        weights = {}
+        for g in range(N_GROUPS):
+            c, half = divmod(g, GROUPS_PER_CHUNK)
+            x_sb = x_pool.tile([P, GT, DM], BF16, name="x_sb")
+            nc.sync.dma_start(out=x_sb[:], in_=chunk_rows(c)[:, half * GT : (half + 1) * GT, :])
+            x_tiles.append(x_sb)
+            if g == 0:
+                weights["txt"] = load_weight(nc, consts, W_eqkv_words, W_eqkv_scales, "txt")
+            if g == 1:
+                weights["img"] = load_weight(nc, consts, W_iqkv_words, W_iqkv_scales, "img")
+            if half == 0:
+                table = table_pool.tile([P, T, 2 * D], BF16, name="table")
+                nc.sync.dma_start(
+                    out=table[:],
+                    in_=image_rotary_emb[c * CHUNK : (c + 1) * CHUNK].rearrange("(p t) i f -> p t (i f)", t=T),
+                )
+                table_tiles.append(table)
+
+        gains = {
+            "txt": load_gains(nc, consts, eqn_scale, ekn_scale, "txt"),
+            "img": load_gains(nc, consts, qn_scale, kn_scale, "img"),
+        }
+        ident = consts.tile([P, P], F32, name="ident")
+        make_identity(nc, ident[:])
+        eps = consts.tile([P, 1], F32, name="eps")
+        nc.vector.memset(eps[:], EPS)
+
+        state = {}
+
+        def stream_of(g):
+            return "txt" if g // GROUPS_PER_CHUNK < TXT_CHUNKS else "img"
+
+        def transpose_and_quantise(g):
+            x_words = x_tiles[g][:].bitcast(F32)
+            grouped = work.tile([P, GT, P, 4], BF16, name="grouped", align_bytes=64)
+            grouped_words = grouped[:].bitcast(F32)
+            for pair in range(GT // 2):
+                xt = xt_psum.tile([P, 2, 2, P], F32, name="xt")
+                for j in range(2):
+                    for u in range(2):
+                        nc.tensor.transpose(xt[:, j, u, :], x_words[:, 2 * pair + j, u : DM // 2 : 2], ident[:])
+                nc.scalar.copy(
+                    out=grouped_words[:, 2 * pair : 2 * pair + 2, :, :],
+                    in_=xt[:].rearrange("p j u r -> p j r u"),
+                )
+            codes = work.tile([P, GT * P], U32, name="codes", align_bytes=64)
+            x_plane = work.tile([P, GT * P], U8, name="x_plane", align_bytes=64)
+            nc.vector.quantize_mx(
+                out=codes[:].bitcast(FP8X4),
+                scales=x_plane[:],
+                in_=grouped[:].rearrange("p j r t -> p (j r t)"),
+            )
+            state["codes", g] = codes
+            state["x_plane", g] = x_plane
+
+        def scale_table(g):
+            c, half = divmod(g, GROUPS_PER_CHUNK)
+            scaled = deep.tile([P, GT, 2, 2 * D], F32, name="scaled")
+            nc.gpsimd.tensor_tensor(
+                out=scaled[:],
+                in0=table_tiles[c][:, half * GT : (half + 1) * GT, :]
+                .rearrange("p t (o f) -> p t o f", o=1)
+                .to_broadcast([P, GT, 2, 2 * D]),
+                in1=gains[stream_of(g)][:].rearrange("p (o q) f -> p o q f", o=1).to_broadcast([P, GT, 2, 2 * D]),
+                op=ALU.mult,
+            )
+            state["scaled", g] = scaled
+
+        def project(g):
+            codes = state["codes", g]
+            x_plane = state["x_plane", g]
+            w_words, w_plane = weights[stream_of(g)]
+            c, half = divmod(g, GROUPS_PER_CHUNK)
+            qk_tiles = []
+            v_ps = v_psum.tile([P, GT, HD], F32, name="v_ps")
+            for pair in range(GT // 2):
+                qk_ps = qk_psum.tile([P, 2, N_QK], F32, name="qk_ps")
+                qk_tiles.append(qk_ps)
+                for j in range(2):
+                    block = slice((2 * pair + j) * P, (2 * pair + j + 1) * P)
+                    nc.tensor.matmul_mx(
+                        out=qk_ps[:, j, :],
+                        lhsT=codes[:, block].bitcast(FP8X4),
+                        lhsT_scale=x_plane[:, block],
+                        rhs=w_words[:, 0 : 2 * N_QK].bitcast(FP4X4),
+                        rhs_scale=w_plane[:, 0:N_QK],
+                        start=True,
+                        stop=True,
+                    )
+                    nc.tensor.matmul_mx(
+                        out=v_ps[:, 2 * pair + j, :],
+                        lhsT=codes[:, block].bitcast(FP8X4),
+                        lhsT_scale=x_plane[:, block],
+                        rhs=w_words[:, 2 * N_QK : 2 * N_QKV].bitcast(FP4X4),
+                        rhs_scale=w_plane[:, N_QK:N_QKV],
+                        start=True,
+                        stop=True,
+                    )
+            squares = work.tile([P, GT, NORMS, D], BF16, name="squares")
+            sums = deep.tile([P, GT * NORMS], F32, name="sums")
+            for j in range(GT):
+                for n in range(NORMS):
+                    nc.scalar.activation(
+                        out=squares[:, j, n, :],
+                        in_=qk_tiles[j // 2][:, j % 2, n * D : (n + 1) * D],
+                        func=ACT.Square,
+                        accum_out=sums[:, j * NORMS + n : j * NORMS + n + 1],
+                    )
+            rms = deep.tile([P, GT * NORMS], F32, name="rms")
+            nc.scalar.activation(out=rms[:], in_=sums[:], func=ACT.Sqrt, bias=eps[:], scale=1.0 / D)
+            if half == 0:
+                state["v_sb", c] = deep.tile([P, T, HD], F32, name="v_sb")
+            nc.scalar.copy(out=state["v_sb", c][:, half * GT : (half + 1) * GT, :], in_=v_ps[:])
+            state["qk", g] = qk_tiles
+            state["rms", g] = rms
+
+        def norm_and_rotate(g):
+            qk_tiles = state["qk", g]
+            rms = state["rms", g]
+            scaled = state["scaled", g]
+            c, half = divmod(g, GROUPS_PER_CHUNK)
+            inv_rms = deep.tile([P, GT * NORMS], F32, name="inv_rms")
+            nc.vector.reciprocal(out=inv_rms[:], in_=rms[:])
+            terms = work.tile([P, 2, 2, GT, HD], F32, name="terms")
+            for j in range(GT):
+                for n in range(NORMS):
+                    qk, head = divmod(n, HEADS)
+                    y = qk_tiles[j // 2][:, j % 2, n * D : (n + 1) * D].rearrange("p (i b) -> p i b", b=2)
+                    f = scaled[:, j, qk, :].rearrange("p (i a b) -> p i a b", a=2, b=2)
+                    for b in range(2):
+                        nc.vector.scalar_tensor_tensor(
+                            out=terms[:, b, qk, j, head * D : (head + 1) * D].rearrange("p (i a) -> p i a", a=2),
+                            in0=y[:, :, b : b + 1].to_broadcast([P, D // 2, 2]),
+                            scalar=inv_rms[:, j * NORMS + n : j * NORMS + n + 1],
+                            in1=f[:, :, :, b],
+                            op0=ALU.mult,
+                            op1=ALU.mult,
+                        )
+            if half == 0:
+                state["rotated", c] = deep.tile([P, 2, T, HD], F32, name="rotated")
+            rotated = state["rotated", c]
+            blocks = slice(half * GT, (half + 1) * GT)
+            nc.vector.tensor_tensor(out=rotated[:, 0, blocks, :], in0=terms[:, 0, 0], in1=terms[:, 1, 0], op=ALU.add)
+            nc.gpsimd.tensor_tensor(out=rotated[:, 1, blocks, :], in0=terms[:, 0, 1], in1=terms[:, 1, 1], op=ALU.add)
+            if half == GROUPS_PER_CHUNK - 1:
+                rows = slice(c * CHUNK, (c + 1) * CHUNK)
+                v_sb = state["v_sb", c]
+                nc.sync.dma_start(out=out_2[0, rows, :].rearrange("(p t) f -> p t f", t=T), in_=v_sb[:])
+                nc.sync.dma_start(out=out_0[0, rows, :].rearrange("(p t) f -> p t f", t=T), in_=rotated[:, 0])
+                nc.sync.dma_start(out=out_1[0, rows, :].rearrange("(p t) f -> p t f", t=T), in_=rotated[:, 1])
+
+        for step in range(N_GROUPS + 2):
+            if step < N_GROUPS:
+                transpose_and_quantise(step)
+                scale_table(step)
+            if 1 <= step <= N_GROUPS:
+                project(step - 1)
+            if step >= 2:
+                norm_and_rotate(step - 2)

@@ -50,16 +50,10 @@ def load_weight(nc, consts, words_dram, scales_dram, label):
 
 
 def load_gains(nc, consts, q_gain, k_gain, label):
-    raw = consts.tile([P, 2, D], BF16, name=label + "_gain")
-    nc.scalar.dma_start(out=raw[:, 0, :], in_=q_gain.partition_broadcast(P))
-    nc.scalar.dma_start(out=raw[:, 1, :], in_=k_gain.partition_broadcast(P))
-    spread = consts.tile([P, 2, 2 * D], BF16, name=label + "_gain_spread")
-    for qk in range(2):
-        nc.vector.tensor_copy(
-            out=spread[:, qk, :].rearrange("p (i a b) -> p i a b", a=2, b=2),
-            in_=raw[:, qk, :].rearrange("p (i o b) -> p i o b", o=1, b=2).to_broadcast([P, D // 2, 2, 2]),
-        )
-    return spread
+    gain = consts.tile([P, 2, D], BF16, name=label + "_gain")
+    nc.scalar.dma_start(out=gain[:, 0, :], in_=q_gain.partition_broadcast(P))
+    nc.scalar.dma_start(out=gain[:, 1, :], in_=k_gain.partition_broadcast(P))
+    return gain
 
 
 def tile_fluxattention_pa_t_kernel(
@@ -155,18 +149,20 @@ def tile_fluxattention_pa_t_kernel(
             state["codes", g] = codes
             state["x_plane", g] = x_plane
 
-        def scale_table(g):
-            c, half = divmod(g, GROUPS_PER_CHUNK)
-            scaled = deep.tile([P, GT, 2, 2 * D], F32, name="scaled")
-            nc.gpsimd.tensor_tensor(
-                out=scaled[:],
-                in0=table_tiles[c][:, half * GT : (half + 1) * GT, :]
-                .rearrange("p t (o f) -> p t o f", o=1)
-                .to_broadcast([P, GT, 2, 2 * D]),
-                in1=gains[stream_of(g)][:].rearrange("p (o q) f -> p o q f", o=1).to_broadcast([P, GT, 2, 2 * D]),
-                op=ALU.mult,
-            )
-            state["scaled", g] = scaled
+        def scale_table(c):
+            stream = "txt" if c < TXT_CHUNKS else "img"
+            table = table_tiles[c][:].rearrange("p t (i a b) -> p t i a b", a=2, b=2)
+            scaled = deep.tile([P, T, 2, 2, D], F32, name="scaled")
+            for qk in range(2):
+                gain = gains[stream][:, qk, :].rearrange("p (o i b) -> p o i b", o=1, b=2)
+                for a in range(2):
+                    nc.gpsimd.tensor_tensor(
+                        out=scaled[:, :, qk, a, :].rearrange("p t (i b) -> p t i b", b=2),
+                        in0=table[:, :, :, a, :],
+                        in1=gain.to_broadcast([P, T, D // 2, 2]),
+                        op=ALU.mult,
+                    )
+            state["scaled", c] = scaled
 
         def project(g):
             codes = state["codes", g]
@@ -219,31 +215,35 @@ def tile_fluxattention_pa_t_kernel(
         def norm_and_rotate(g):
             qk_tiles = state["qk", g]
             rms = state["rms", g]
-            scaled = state["scaled", g]
             c, half = divmod(g, GROUPS_PER_CHUNK)
+            scaled = state["scaled", c]
             inv_rms = deep.tile([P, GT * NORMS], F32, name="inv_rms")
             nc.vector.reciprocal(out=inv_rms[:], in_=rms[:])
-            terms = work.tile([P, 2, 2, GT, HD], F32, name="terms")
+            terms = work.tile([P, 2, GT, HEADS, 2, D], F32, name="terms")
             for j in range(GT):
                 for n in range(NORMS):
                     qk, head = divmod(n, HEADS)
-                    y = qk_tiles[j // 2][:, j % 2, n * D : (n + 1) * D].rearrange("p (i b) -> p i b", b=2)
-                    f = scaled[:, j, qk, :].rearrange("p (i a b) -> p i a b", a=2, b=2)
-                    for b in range(2):
-                        nc.vector.scalar_tensor_tensor(
-                            out=terms[:, b, qk, j, head * D : (head + 1) * D].rearrange("p (i a) -> p i a", a=2),
-                            in0=y[:, :, b : b + 1].to_broadcast([P, D // 2, 2]),
-                            scalar=inv_rms[:, j * NORMS + n : j * NORMS + n + 1],
-                            in1=f[:, :, :, b],
-                            op0=ALU.mult,
-                            op1=ALU.mult,
-                        )
+                    y = qk_tiles[j // 2][:, j % 2, n * D : (n + 1) * D].rearrange("p (o f) -> p o f", o=1)
+                    nc.vector.scalar_tensor_tensor(
+                        out=terms[:, qk, j, head],
+                        in0=y.to_broadcast([P, 2, D]),
+                        scalar=inv_rms[:, j * NORMS + n : j * NORMS + n + 1],
+                        in1=scaled[:, half * GT + j, qk],
+                        op0=ALU.mult,
+                        op1=ALU.mult,
+                    )
             if half == 0:
                 state["rotated", c] = deep.tile([P, 2, T, HD], F32, name="rotated")
             rotated = state["rotated", c]
             blocks = slice(half * GT, (half + 1) * GT)
-            nc.vector.tensor_tensor(out=rotated[:, 0, blocks, :], in0=terms[:, 0, 0], in1=terms[:, 1, 0], op=ALU.add)
-            nc.gpsimd.tensor_tensor(out=rotated[:, 1, blocks, :], in0=terms[:, 0, 1], in1=terms[:, 1, 1], op=ALU.add)
+            for qk, engine in ((0, nc.vector), (1, nc.gpsimd)):
+                pairs = terms[:, qk].rearrange("p j h a (i b) -> p (j h) i a b", b=2)
+                engine.tensor_tensor(
+                    out=rotated[:, qk, blocks, :].rearrange("p j (h i a) -> p (j h) i a", h=HEADS, a=2),
+                    in0=pairs[:, :, :, :, 0],
+                    in1=pairs[:, :, :, :, 1],
+                    op=ALU.add,
+                )
             if half == GROUPS_PER_CHUNK - 1:
                 rows = slice(c * CHUNK, (c + 1) * CHUNK)
                 v_sb = state["v_sb", c]
@@ -254,7 +254,8 @@ def tile_fluxattention_pa_t_kernel(
         for step in range(N_GROUPS + 2):
             if step < N_GROUPS:
                 transpose_and_quantise(step)
-                scale_table(step)
+                if step % GROUPS_PER_CHUNK == 0:
+                    scale_table(step // GROUPS_PER_CHUNK)
             if 1 <= step <= N_GROUPS:
                 project(step - 1)
             if step >= 2:

@@ -236,9 +236,9 @@ def tile_fluxattention_pa_t_kernel(
                 state["rotated", c] = deep.tile([P, 2, T, HD], F32, name="rotated")
             rotated = state["rotated", c]
             blocks = slice(half * GT, (half + 1) * GT)
-            for qk, engine in ((0, nc.vector), (1, nc.gpsimd)):
+            for qk in range(2):
                 pairs = terms[:, qk].rearrange("p j h a (i b) -> p (j h) i a b", b=2)
-                engine.tensor_tensor(
+                nc.vector.tensor_tensor(
                     out=rotated[:, qk, blocks, :].rearrange("p j (h i a) -> p (j h) i a", h=HEADS, a=2),
                     in0=pairs[:, :, :, :, 0],
                     in1=pairs[:, :, :, :, 1],

@@ -28,7 +28,8 @@ T = 8
 CHUNK = P * T
 N_CHUNKS = (L_TXT + L_IMG) // CHUNK
 TXT_CHUNKS = L_TXT // CHUNK
-GT = 4
+GT = 2
+XB = 4
 GROUPS_PER_CHUNK = T // GT
 N_GROUPS = N_CHUNKS * GROUPS_PER_CHUNK
 NORMS = 2 * HEADS
@@ -76,9 +77,9 @@ def tile_fluxattention_pa_t_kernel(
     nc = tc.nc
     with ExitStack() as ctx:
         consts = ctx.enter_context(tc.tile_pool(name="consts", bufs=1))
-        x_pool = ctx.enter_context(tc.tile_pool(name="x", bufs=N_GROUPS))
+        x_pool = ctx.enter_context(tc.tile_pool(name="x", bufs=N_CHUNKS * T // XB))
         table_pool = ctx.enter_context(tc.tile_pool(name="table", bufs=N_CHUNKS))
-        work = ctx.enter_context(tc.tile_pool(name="work", bufs=2))
+        work = ctx.enter_context(tc.tile_pool(name="work", bufs=3))
         deep = ctx.enter_context(tc.tile_pool(name="deep", bufs=3))
         xt_psum = ctx.enter_context(tc.psum_pool(name="xt_psum", bufs=2))
         qk_psum = ctx.enter_context(tc.psum_pool(name="qk_psum", bufs=4))
@@ -95,22 +96,22 @@ def tile_fluxattention_pa_t_kernel(
         x_tiles = []
         table_tiles = []
         weights = {}
-        for g in range(N_GROUPS):
-            c, half = divmod(g, GROUPS_PER_CHUNK)
-            x_sb = x_pool.tile([P, GT, DM], BF16, name="x_sb")
-            nc.sync.dma_start(out=x_sb[:], in_=chunk_rows(c)[:, half * GT : (half + 1) * GT, :])
-            x_tiles.append(x_sb)
-            if g == 0:
-                weights["txt"] = load_weight(nc, consts, W_eqkv_words, W_eqkv_scales, "txt")
-            if g == 1:
-                weights["img"] = load_weight(nc, consts, W_iqkv_words, W_iqkv_scales, "img")
-            if half == 0:
-                table = table_pool.tile([P, T, 2 * D], BF16, name="table")
-                nc.sync.dma_start(
-                    out=table[:],
-                    in_=image_rotary_emb[c * CHUNK : (c + 1) * CHUNK].rearrange("(p t) i f -> p t (i f)", t=T),
-                )
-                table_tiles.append(table)
+        for c in range(N_CHUNKS):
+            for part in range(T // XB):
+                x_sb = x_pool.tile([P, XB, DM], BF16, name="x_sb")
+                nc.sync.dma_start(out=x_sb[:], in_=chunk_rows(c)[:, part * XB : (part + 1) * XB, :])
+                x_tiles.append(x_sb)
+                if part == 0:
+                    table = table_pool.tile([P, T, 2 * D], BF16, name="table")
+                    nc.sync.dma_start(
+                        out=table[:],
+                        in_=image_rotary_emb[c * CHUNK : (c + 1) * CHUNK].rearrange("(p t) i f -> p t (i f)", t=T),
+                    )
+                    table_tiles.append(table)
+                    if c == 0:
+                        weights["txt"] = load_weight(nc, consts, W_eqkv_words, W_eqkv_scales, "txt")
+                    if c == 1:
+                        weights["img"] = load_weight(nc, consts, W_iqkv_words, W_iqkv_scales, "img")
 
         gains = {
             "txt": load_gains(nc, consts, eqn_scale, ekn_scale, "txt"),
@@ -127,14 +128,15 @@ def tile_fluxattention_pa_t_kernel(
             return "txt" if g // GROUPS_PER_CHUNK < TXT_CHUNKS else "img"
 
         def transpose_and_quantise(g):
-            x_words = x_tiles[g][:].bitcast(F32)
+            load, first = divmod(g * GT, XB)
+            x_words = x_tiles[load][:].bitcast(F32)
             grouped = work.tile([P, GT, P, 4], BF16, name="grouped", align_bytes=64)
             grouped_words = grouped[:].bitcast(F32)
             for pair in range(GT // 2):
                 xt = xt_psum.tile([P, 2, 2, P], F32, name="xt")
                 for j in range(2):
                     for u in range(2):
-                        nc.tensor.transpose(xt[:, j, u, :], x_words[:, 2 * pair + j, u : DM // 2 : 2], ident[:])
+                        nc.tensor.transpose(xt[:, j, u, :], x_words[:, first + 2 * pair + j, u : DM // 2 : 2], ident[:])
                 nc.scalar.copy(
                     out=grouped_words[:, 2 * pair : 2 * pair + 2, :, :],
                     in_=xt[:].rearrange("p j u r -> p j r u"),
@@ -149,20 +151,16 @@ def tile_fluxattention_pa_t_kernel(
             state["codes", g] = codes
             state["x_plane", g] = x_plane
 
-        def scale_table(c):
+        def scale_table(engine, c, qk, a):
             stream = "txt" if c < TXT_CHUNKS else "img"
-            table = table_tiles[c][:].rearrange("p t (i a b) -> p t i a b", a=2, b=2)
-            scaled = deep.tile([P, T, 2, 2, D], F32, name="scaled")
-            for qk in range(2):
-                gain = gains[stream][:, qk, :].rearrange("p (o i b) -> p o i b", o=1, b=2)
-                for a in range(2):
-                    nc.gpsimd.tensor_tensor(
-                        out=scaled[:, :, qk, a, :].rearrange("p t (i b) -> p t i b", b=2),
-                        in0=table[:, :, :, a, :],
-                        in1=gain.to_broadcast([P, T, D // 2, 2]),
-                        op=ALU.mult,
-                    )
-            state["scaled", c] = scaled
+            if qk == 0 and a == 0:
+                state["scaled", c] = deep.tile([P, T, 2, 2, D], F32, name="scaled")
+            engine.tensor_tensor(
+                out=state["scaled", c][:, :, qk, a, :].rearrange("p t (i b) -> p t i b", b=2),
+                in0=table_tiles[c][:].rearrange("p t (i a b) -> p t i a b", a=2, b=2)[:, :, :, a, :],
+                in1=gains[stream][:, qk, :].rearrange("p (o i b) -> p o i b", o=1, b=2).to_broadcast([P, T, D // 2, 2]),
+                op=ALU.mult,
+            )
 
         def project(g):
             codes = state["codes", g]
@@ -204,21 +202,29 @@ def tile_fluxattention_pa_t_kernel(
                         func=ACT.Square,
                         accum_out=sums[:, j * NORMS + n : j * NORMS + n + 1],
                     )
-            rms = deep.tile([P, GT * NORMS], F32, name="rms")
-            nc.scalar.activation(out=rms[:], in_=sums[:], func=ACT.Sqrt, bias=eps[:], scale=1.0 / D)
             if half == 0:
                 state["v_sb", c] = deep.tile([P, T, HD], F32, name="v_sb")
-            nc.scalar.copy(out=state["v_sb", c][:, half * GT : (half + 1) * GT, :], in_=v_ps[:])
+            v_sb = state["v_sb", c]
+            nc.scalar.copy(out=v_sb[:, half * GT : (half + 1) * GT, :], in_=v_ps[:])
+            if half == GROUPS_PER_CHUNK - 1:
+                nc.sync.dma_start(
+                    out=out_2[0, c * CHUNK : (c + 1) * CHUNK, :].rearrange("(p t) f -> p t f", t=T), in_=v_sb[:]
+                )
+            rms = deep.tile([P, GT * NORMS], F32, name="rms")
+            nc.scalar.activation(out=rms[:], in_=sums[:], func=ACT.Sqrt, bias=eps[:], scale=1.0 / D)
             state["qk", g] = qk_tiles
             state["rms", g] = rms
 
-        def norm_and_rotate(g):
+        def invert_rms(g):
+            inv_rms = deep.tile([P, GT * NORMS], F32, name="inv_rms")
+            nc.vector.reciprocal(out=inv_rms[:], in_=state["rms", g][:])
+            state["inv_rms", g] = inv_rms
+
+        def multiply(g):
             qk_tiles = state["qk", g]
-            rms = state["rms", g]
+            inv_rms = state["inv_rms", g]
             c, half = divmod(g, GROUPS_PER_CHUNK)
             scaled = state["scaled", c]
-            inv_rms = deep.tile([P, GT * NORMS], F32, name="inv_rms")
-            nc.vector.reciprocal(out=inv_rms[:], in_=rms[:])
             terms = work.tile([P, 2, GT, HEADS, 2, D], F32, name="terms")
             for j in range(GT):
                 for n in range(NORMS):
@@ -232,13 +238,18 @@ def tile_fluxattention_pa_t_kernel(
                         op0=ALU.mult,
                         op1=ALU.mult,
                     )
+            state["terms", g] = terms
+
+        def add_terms(g):
+            terms = state["terms", g]
+            c, half = divmod(g, GROUPS_PER_CHUNK)
             if half == 0:
                 state["rotated", c] = deep.tile([P, 2, T, HD], F32, name="rotated")
             rotated = state["rotated", c]
             blocks = slice(half * GT, (half + 1) * GT)
-            for qk in range(2):
+            for qk, engine in ((0, nc.vector), (1, nc.gpsimd if g % 2 == 0 else nc.vector)):
                 pairs = terms[:, qk].rearrange("p j h a (i b) -> p (j h) i a b", b=2)
-                nc.vector.tensor_tensor(
+                engine.tensor_tensor(
                     out=rotated[:, qk, blocks, :].rearrange("p j (h i a) -> p (j h) i a", h=HEADS, a=2),
                     in0=pairs[:, :, :, :, 0],
                     in1=pairs[:, :, :, :, 1],
@@ -246,17 +257,22 @@ def tile_fluxattention_pa_t_kernel(
                 )
             if half == GROUPS_PER_CHUNK - 1:
                 rows = slice(c * CHUNK, (c + 1) * CHUNK)
-                v_sb = state["v_sb", c]
-                nc.sync.dma_start(out=out_2[0, rows, :].rearrange("(p t) f -> p t f", t=T), in_=v_sb[:])
                 nc.sync.dma_start(out=out_0[0, rows, :].rearrange("(p t) f -> p t f", t=T), in_=rotated[:, 0])
                 nc.sync.dma_start(out=out_1[0, rows, :].rearrange("(p t) f -> p t f", t=T), in_=rotated[:, 1])
 
-        for step in range(N_GROUPS + 2):
+        for quarter in range(GROUPS_PER_CHUNK):
+            scale_table(nc.vector, 0, quarter // 2, quarter % 2)
+        for step in range(N_GROUPS + 3):
+            c, quarter = divmod(step, GROUPS_PER_CHUNK)
+            if 2 <= step < N_GROUPS + 2:
+                invert_rms(step - 2)
             if step < N_GROUPS:
                 transpose_and_quantise(step)
-                if step % GROUPS_PER_CHUNK == 0:
-                    scale_table(step // GROUPS_PER_CHUNK)
-            if 1 <= step <= N_GROUPS:
+            if c + 1 < N_CHUNKS:
+                scale_table(nc.gpsimd, c + 1, quarter // 2, quarter % 2)
+            if 1 <= step < N_GROUPS + 1:
                 project(step - 1)
-            if step >= 2:
-                norm_and_rotate(step - 2)
+            if step >= 3:
+                add_terms(step - 3)
+            if 2 <= step < N_GROUPS + 2:
+                multiply(step - 2)

@@ -205,7 +205,7 @@ def tile_fluxattention_pa_t_kernel(
             if half == 0:
                 state["v_sb", c] = deep.tile([P, T, HD], F32, name="v_sb")
             v_sb = state["v_sb", c]
-            nc.scalar.copy(out=v_sb[:, half * GT : (half + 1) * GT, :], in_=v_ps[:])
+            nc.vector.tensor_copy(out=v_sb[:, half * GT : (half + 1) * GT, :], in_=v_ps[:])
             if half == GROUPS_PER_CHUNK - 1:
                 nc.sync.dma_start(
                     out=out_2[0, c * CHUNK : (c + 1) * CHUNK, :].rearrange("(p t) f -> p t f", t=T), in_=v_sb[:]

@@ -22,6 +22,7 @@ D = 64
 HD = HEADS * D
 N_QK = 2 * HD
 N_QKV = 3 * HD
+N_PASS = 512
 EPS = 1e-6
 
 T = 8
@@ -38,13 +39,14 @@ FLOPS = 2 * (L_TXT + L_IMG) * DM * N_QKV
 
 
 def load_weight(nc, consts, words_dram, scales_dram, label):
-    words = consts.tile([P, 2 * N_QKV], U8, name=label + "_words", align_bytes=64)
-    nc.sync.dma_start(out=words[:].bitcast(I32), in_=words_dram[0].bitcast(I32))
-    plane = consts.tile([P, N_QKV], U8, name=label + "_plane", align_bytes=64)
+    words = consts.tile([P, 2 * N_PASS], U8, name=label + "_words", align_bytes=64)
+    nc.vector.memset(words[:, 2 * N_QKV :].bitcast(I32), 0)
+    nc.sync.dma_start(out=words[:, : 2 * N_QKV].bitcast(I32), in_=words_dram[0].bitcast(I32))
+    plane = consts.tile([P, N_PASS], U8, name=label + "_plane", align_bytes=64)
     nc.vector.memset(plane[:].bitcast(I32), 0)
     for quadrant in range(4):
         nc.sync.dma_start(
-            out=plane[32 * quadrant : 32 * quadrant + 4, :].bitcast(I32),
+            out=plane[32 * quadrant : 32 * quadrant + 4, :N_QKV].bitcast(I32),
             in_=scales_dram[0, 4 * quadrant : 4 * quadrant + 4, :].bitcast(I32),
         )
     return words, plane
@@ -82,8 +84,7 @@ def tile_fluxattention_pa_t_kernel(
         work = ctx.enter_context(tc.tile_pool(name="work", bufs=3))
         deep = ctx.enter_context(tc.tile_pool(name="deep", bufs=3))
         xt_psum = ctx.enter_context(tc.psum_pool(name="xt_psum", bufs=2))
-        qk_psum = ctx.enter_context(tc.psum_pool(name="qk_psum", bufs=4))
-        v_psum = ctx.enter_context(tc.psum_pool(name="v_psum", bufs=2))
+        y_psum = ctx.enter_context(tc.psum_pool(name="y_psum", bufs=6))
         ctx.enter_context(tc.manual_schedule())
 
         def chunk_rows(c):
@@ -167,52 +168,41 @@ def tile_fluxattention_pa_t_kernel(
             x_plane = state["x_plane", g]
             w_words, w_plane = weights[stream_of(g)]
             c, half = divmod(g, GROUPS_PER_CHUNK)
-            qk_tiles = []
-            v_ps = v_psum.tile([P, GT, HD], F32, name="v_ps")
-            for pair in range(GT // 2):
-                qk_ps = qk_psum.tile([P, 2, N_QK], F32, name="qk_ps")
-                qk_tiles.append(qk_ps)
-                for j in range(2):
-                    block = slice((2 * pair + j) * P, (2 * pair + j + 1) * P)
-                    nc.tensor.matmul_mx(
-                        out=qk_ps[:, j, :],
-                        lhsT=codes[:, block].bitcast(FP8X4),
-                        lhsT_scale=x_plane[:, block],
-                        rhs=w_words[:, 0 : 2 * N_QK].bitcast(FP4X4),
-                        rhs_scale=w_plane[:, 0:N_QK],
-                        start=True,
-                        stop=True,
-                    )
-                    nc.tensor.matmul_mx(
-                        out=v_ps[:, 2 * pair + j, :],
-                        lhsT=codes[:, block].bitcast(FP8X4),
-                        lhsT_scale=x_plane[:, block],
-                        rhs=w_words[:, 2 * N_QK : 2 * N_QKV].bitcast(FP4X4),
-                        rhs_scale=w_plane[:, N_QK:N_QKV],
-                        start=True,
-                        stop=True,
-                    )
+            y_tiles = []
+            for j in range(GT):
+                y_ps = y_psum.tile([P, N_PASS], F32, name="y_ps")
+                y_tiles.append(y_ps)
+                nc.tensor.matmul_mx(
+                    out=y_ps[:],
+                    lhsT=codes[:, j * P : (j + 1) * P].bitcast(FP8X4),
+                    lhsT_scale=x_plane[:, j * P : (j + 1) * P],
+                    rhs=w_words[:].bitcast(FP4X4),
+                    rhs_scale=w_plane[:],
+                    start=True,
+                    stop=True,
+                )
             squares = work.tile([P, GT, NORMS, D], BF16, name="squares")
             sums = deep.tile([P, GT * NORMS], F32, name="sums")
             for j in range(GT):
                 for n in range(NORMS):
                     nc.scalar.activation(
                         out=squares[:, j, n, :],
-                        in_=qk_tiles[j // 2][:, j % 2, n * D : (n + 1) * D],
+                        in_=y_tiles[j][:, n * D : (n + 1) * D],
                         func=ACT.Square,
                         accum_out=sums[:, j * NORMS + n : j * NORMS + n + 1],
                     )
             if half == 0:
                 state["v_sb", c] = deep.tile([P, T, HD], F32, name="v_sb")
             v_sb = state["v_sb", c]
-            nc.vector.tensor_copy(out=v_sb[:, half * GT : (half + 1) * GT, :], in_=v_ps[:])
+            for j in range(GT):
+                nc.scalar.copy(out=v_sb[:, half * GT + j, :], in_=y_tiles[j][:, N_QK:N_QKV])
             if half == GROUPS_PER_CHUNK - 1:
                 nc.sync.dma_start(
                     out=out_2[0, c * CHUNK : (c + 1) * CHUNK, :].rearrange("(p t) f -> p t f", t=T), in_=v_sb[:]
                 )
             rms = deep.tile([P, GT * NORMS], F32, name="rms")
             nc.scalar.activation(out=rms[:], in_=sums[:], func=ACT.Sqrt, bias=eps[:], scale=1.0 / D)
-            state["qk", g] = qk_tiles
+            state["y", g] = y_tiles
             state["rms", g] = rms
 
         def invert_rms(g):
@@ -221,7 +211,7 @@ def tile_fluxattention_pa_t_kernel(
             state["inv_rms", g] = inv_rms
 
         def multiply(g):
-            qk_tiles = state["qk", g]
+            y_tiles = state["y", g]
             inv_rms = state["inv_rms", g]
             c, half = divmod(g, GROUPS_PER_CHUNK)
             scaled = state["scaled", c]
@@ -229,7 +219,7 @@ def tile_fluxattention_pa_t_kernel(
             for j in range(GT):
                 for n in range(NORMS):
                     qk, head = divmod(n, HEADS)
-                    y = qk_tiles[j // 2][:, j % 2, n * D : (n + 1) * D].rearrange("p (o f) -> p o f", o=1)
+                    y = y_tiles[j][:, n * D : (n + 1) * D].rearrange("p (o f) -> p o f", o=1)
                     nc.vector.scalar_tensor_tensor(
                         out=terms[:, qk, j, head],
                         in0=y.to_broadcast([P, 2, D]),

@@ -237,9 +237,9 @@ def tile_fluxattention_pa_t_kernel(
                 state["rotated", c] = deep.tile([P, 2, T, HD], F32, name="rotated")
             rotated = state["rotated", c]
             blocks = slice(half * GT, (half + 1) * GT)
-            for qk, engine in ((0, nc.vector), (1, nc.gpsimd if g % 2 == 0 else nc.vector)):
+            for qk in range(2):
                 pairs = terms[:, qk].rearrange("p j h a (i b) -> p (j h) i a b", b=2)
-                engine.tensor_tensor(
+                nc.vector.tensor_tensor(
                     out=rotated[:, qk, blocks, :].rearrange("p j (h i a) -> p (j h) i a", h=HEADS, a=2),
                     in0=pairs[:, :, :, :, 0],
                     in1=pairs[:, :, :, :, 1],

@@ -152,11 +152,11 @@ def tile_fluxattention_pa_t_kernel(
             state["codes", g] = codes
             state["x_plane", g] = x_plane
 
-        def scale_table(engine, c, qk, a):
+        def scale_table(c, qk, a):
             stream = "txt" if c < TXT_CHUNKS else "img"
             if qk == 0 and a == 0:
                 state["scaled", c] = deep.tile([P, T, 2, 2, D], F32, name="scaled")
-            engine.tensor_tensor(
+            nc.vector.tensor_tensor(
                 out=state["scaled", c][:, :, qk, a, :].rearrange("p t (i b) -> p t i b", b=2),
                 in0=table_tiles[c][:].rearrange("p t (i a b) -> p t i a b", a=2, b=2)[:, :, :, a, :],
                 in1=gains[stream][:, qk, :].rearrange("p (o i b) -> p o i b", o=1, b=2).to_broadcast([P, T, D // 2, 2]),
@@ -200,14 +200,9 @@ def tile_fluxattention_pa_t_kernel(
                 nc.sync.dma_start(
                     out=out_2[0, c * CHUNK : (c + 1) * CHUNK, :].rearrange("(p t) f -> p t f", t=T), in_=v_sb[:]
                 )
-            rms = deep.tile([P, GT * NORMS], F32, name="rms")
-            nc.scalar.activation(out=rms[:], in_=sums[:], func=ACT.Sqrt, bias=eps[:], scale=1.0 / D)
-            state["y", g] = y_tiles
-            state["rms", g] = rms
-
-        def invert_rms(g):
             inv_rms = deep.tile([P, GT * NORMS], F32, name="inv_rms")
-            nc.vector.reciprocal(out=inv_rms[:], in_=state["rms", g][:])
+            nc.scalar.activation(out=inv_rms[:], in_=sums[:], func=ACT.Abs_reciprocal_sqrt, bias=eps[:], scale=1.0 / D)
+            state["y", g] = y_tiles
             state["inv_rms", g] = inv_rms
 
         def multiply(g):
@@ -239,7 +234,7 @@ def tile_fluxattention_pa_t_kernel(
             blocks = slice(half * GT, (half + 1) * GT)
             for qk in range(2):
                 pairs = terms[:, qk].rearrange("p j h a (i b) -> p (j h) i a b", b=2)
-                nc.vector.tensor_tensor(
+                nc.gpsimd.tensor_tensor(
                     out=rotated[:, qk, blocks, :].rearrange("p j (h i a) -> p (j h) i a", h=HEADS, a=2),
                     in0=pairs[:, :, :, :, 0],
                     in1=pairs[:, :, :, :, 1],
@@ -251,15 +246,13 @@ def tile_fluxattention_pa_t_kernel(
                 nc.sync.dma_start(out=out_1[0, rows, :].rearrange("(p t) f -> p t f", t=T), in_=rotated[:, 1])
 
         for quarter in range(GROUPS_PER_CHUNK):
-            scale_table(nc.vector, 0, quarter // 2, quarter % 2)
+            scale_table(0, quarter // 2, quarter % 2)
         for step in range(N_GROUPS + 3):
             c, quarter = divmod(step, GROUPS_PER_CHUNK)
-            if 2 <= step < N_GROUPS + 2:
-                invert_rms(step - 2)
             if step < N_GROUPS:
                 transpose_and_quantise(step)
             if c + 1 < N_CHUNKS:
-                scale_table(nc.gpsimd, c + 1, quarter // 2, quarter % 2)
+                scale_table(c + 1, quarter // 2, quarter % 2)
             if 1 <= step < N_GROUPS + 1:
                 project(step - 1)
             if step >= 3:

@@ -84,7 +84,8 @@ def tile_fluxattention_pa_t_kernel(
         work = ctx.enter_context(tc.tile_pool(name="work", bufs=3))
         deep = ctx.enter_context(tc.tile_pool(name="deep", bufs=3))
         xt_psum = ctx.enter_context(tc.psum_pool(name="xt_psum", bufs=2))
-        y_psum = ctx.enter_context(tc.psum_pool(name="y_psum", bufs=6))
+        y_psum = ctx.enter_context(tc.psum_pool(name="y_psum", bufs=5))
+        gain_psum = ctx.enter_context(tc.psum_pool(name="gain_psum", bufs=1))
         ctx.enter_context(tc.manual_schedule())
 
         def chunk_rows(c):
@@ -120,6 +121,10 @@ def tile_fluxattention_pa_t_kernel(
         }
         ident = consts.tile([P, P], F32, name="ident")
         make_identity(nc, ident[:])
+        ident_bf = consts.tile([P, P], BF16, name="ident_bf")
+        make_identity(nc, ident_bf[:])
+        gains_ps = gain_psum.tile([P, 2, 2, D], F32, name="gains_ps")
+        STREAMS = ("txt", "img")
         eps = consts.tile([P, 1], F32, name="eps")
         nc.vector.memset(eps[:], EPS)
 
@@ -158,8 +163,10 @@ def tile_fluxattention_pa_t_kernel(
                 state["scaled", c] = deep.tile([P, T, 2, 2, D], F32, name="scaled")
             nc.vector.tensor_tensor(
                 out=state["scaled", c][:, :, qk, a, :].rearrange("p t (i b) -> p t i b", b=2),
-                in0=table_tiles[c][:].rearrange("p t (i a b) -> p t i a b", a=2, b=2)[:, :, :, a, :],
-                in1=gains[stream][:, qk, :].rearrange("p (o i b) -> p o i b", o=1, b=2).to_broadcast([P, T, D // 2, 2]),
+                in0=gains_ps[:, STREAMS.index(stream), qk, :]
+                .rearrange("p (o i b) -> p o i b", o=1, b=2)
+                .to_broadcast([P, T, D // 2, 2]),
+                in1=table_tiles[c][:].rearrange("p t (i a b) -> p t i a b", a=2, b=2)[:, :, :, a, :],
                 op=ALU.mult,
             )
 
@@ -245,12 +252,21 @@ def tile_fluxattention_pa_t_kernel(
                 nc.sync.dma_start(out=out_0[0, rows, :].rearrange("(p t) f -> p t f", t=T), in_=rotated[:, 0])
                 nc.sync.dma_start(out=out_1[0, rows, :].rearrange("(p t) f -> p t f", t=T), in_=rotated[:, 1])
 
-        for quarter in range(GROUPS_PER_CHUNK):
-            scale_table(0, quarter // 2, quarter % 2)
         for step in range(N_GROUPS + 3):
             c, quarter = divmod(step, GROUPS_PER_CHUNK)
             if step < N_GROUPS:
                 transpose_and_quantise(step)
+            if step == 0:
+                for s, stream in enumerate(STREAMS):
+                    nc.tensor.matmul(
+                        out=gains_ps[:, s].rearrange("p q f -> p (q f)"),
+                        lhsT=ident_bf[:],
+                        rhs=gains[stream][:].rearrange("p q f -> p (q f)"),
+                        start=True,
+                        stop=True,
+                    )
+                for first_quarter in range(GROUPS_PER_CHUNK):
+                    scale_table(0, first_quarter // 2, first_quarter % 2)
             if c + 1 < N_CHUNKS:
                 scale_table(c + 1, quarter // 2, quarter % 2)
             if 1 <= step < N_GROUPS + 1:

@@ -101,8 +101,14 @@ def tile_fluxattention_pa_t_kernel(
         for c in range(N_CHUNKS):
             for part in range(T // XB):
                 x_sb = x_pool.tile([P, XB, DM], BF16, name="x_sb")
-                nc.sync.dma_start(out=x_sb[:], in_=chunk_rows(c)[:, part * XB : (part + 1) * XB, :])
                 x_tiles.append(x_sb)
+                pieces = 2 if c == 0 and part == 0 else 1
+                for piece in range(pieces):
+                    blocks = slice(piece * XB // pieces, (piece + 1) * XB // pieces)
+                    nc.sync.dma_start(
+                        out=x_sb[:, blocks, :],
+                        in_=chunk_rows(c)[:, part * XB + blocks.start : part * XB + blocks.stop, :],
+                    )
                 if part == 0:
                     table = table_pool.tile([P, T, 2 * D], BF16, name="table")
                     nc.sync.dma_start(
@@ -170,6 +176,15 @@ def tile_fluxattention_pa_t_kernel(
                 op=ALU.mult,
             )
 
+        def store(out, tile, g):
+            c, half = divmod(g, GROUPS_PER_CHUNK)
+            rows = out[0, c * CHUNK : (c + 1) * CHUNK, :].rearrange("(p t) f -> p t f", t=T)
+            if c == N_CHUNKS - 1:
+                blocks = slice(half * GT, (half + 1) * GT)
+                nc.sync.dma_start(out=rows[:, blocks, :], in_=tile[:, blocks, :])
+            elif half == GROUPS_PER_CHUNK - 1:
+                nc.sync.dma_start(out=rows, in_=tile[:])
+
         def project(g):
             codes = state["codes", g]
             x_plane = state["x_plane", g]
@@ -198,17 +213,14 @@ def tile_fluxattention_pa_t_kernel(
                         func=ACT.Square,
                         accum_out=sums[:, j * NORMS + n : j * NORMS + n + 1],
                     )
+            inv_rms = deep.tile([P, GT * NORMS], F32, name="inv_rms")
+            nc.scalar.activation(out=inv_rms[:], in_=sums[:], func=ACT.Abs_reciprocal_sqrt, bias=eps[:], scale=1.0 / D)
             if half == 0:
                 state["v_sb", c] = deep.tile([P, T, HD], F32, name="v_sb")
             v_sb = state["v_sb", c]
             for j in range(GT):
                 nc.scalar.copy(out=v_sb[:, half * GT + j, :], in_=y_tiles[j][:, N_QK:N_QKV])
-            if half == GROUPS_PER_CHUNK - 1:
-                nc.sync.dma_start(
-                    out=out_2[0, c * CHUNK : (c + 1) * CHUNK, :].rearrange("(p t) f -> p t f", t=T), in_=v_sb[:]
-                )
-            inv_rms = deep.tile([P, GT * NORMS], F32, name="inv_rms")
-            nc.scalar.activation(out=inv_rms[:], in_=sums[:], func=ACT.Abs_reciprocal_sqrt, bias=eps[:], scale=1.0 / D)
+            store(out_2, v_sb, g)
             state["y", g] = y_tiles
             state["inv_rms", g] = inv_rms
 
@@ -239,18 +251,16 @@ def tile_fluxattention_pa_t_kernel(
                 state["rotated", c] = deep.tile([P, 2, T, HD], F32, name="rotated")
             rotated = state["rotated", c]
             blocks = slice(half * GT, (half + 1) * GT)
-            for qk in range(2):
+            engine = nc.vector if g == N_GROUPS - 1 else nc.gpsimd
+            for qk, out in enumerate((out_0, out_1)):
                 pairs = terms[:, qk].rearrange("p j h a (i b) -> p (j h) i a b", b=2)
-                nc.gpsimd.tensor_tensor(
+                engine.tensor_tensor(
                     out=rotated[:, qk, blocks, :].rearrange("p j (h i a) -> p (j h) i a", h=HEADS, a=2),
                     in0=pairs[:, :, :, :, 0],
                     in1=pairs[:, :, :, :, 1],
                     op=ALU.add,
                 )
-            if half == GROUPS_PER_CHUNK - 1:
-                rows = slice(c * CHUNK, (c + 1) * CHUNK)
-                nc.sync.dma_start(out=out_0[0, rows, :].rearrange("(p t) f -> p t f", t=T), in_=rotated[:, 0])
-                nc.sync.dma_start(out=out_1[0, rows, :].rearrange("(p t) f -> p t f", t=T), in_=rotated[:, 1])
+                store(out, rotated[:, qk], g)
 
         for step in range(N_GROUPS + 3):
             c, quarter = divmod(step, GROUPS_PER_CHUNK)

@@ -101,14 +101,8 @@ def tile_fluxattention_pa_t_kernel(
         for c in range(N_CHUNKS):
             for part in range(T // XB):
                 x_sb = x_pool.tile([P, XB, DM], BF16, name="x_sb")
+                nc.sync.dma_start(out=x_sb[:], in_=chunk_rows(c)[:, part * XB : (part + 1) * XB, :])
                 x_tiles.append(x_sb)
-                pieces = 2 if c == 0 and part == 0 else 1
-                for piece in range(pieces):
-                    blocks = slice(piece * XB // pieces, (piece + 1) * XB // pieces)
-                    nc.sync.dma_start(
-                        out=x_sb[:, blocks, :],
-                        in_=chunk_rows(c)[:, part * XB + blocks.start : part * XB + blocks.stop, :],
-                    )
                 if part == 0:
                     table = table_pool.tile([P, T, 2 * D], BF16, name="table")
                     nc.sync.dma_start(
@@ -213,14 +207,14 @@ def tile_fluxattention_pa_t_kernel(
                         func=ACT.Square,
                         accum_out=sums[:, j * NORMS + n : j * NORMS + n + 1],
                     )
-            inv_rms = deep.tile([P, GT * NORMS], F32, name="inv_rms")
-            nc.scalar.activation(out=inv_rms[:], in_=sums[:], func=ACT.Abs_reciprocal_sqrt, bias=eps[:], scale=1.0 / D)
             if half == 0:
                 state["v_sb", c] = deep.tile([P, T, HD], F32, name="v_sb")
             v_sb = state["v_sb", c]
             for j in range(GT):
                 nc.scalar.copy(out=v_sb[:, half * GT + j, :], in_=y_tiles[j][:, N_QK:N_QKV])
             store(out_2, v_sb, g)
+            inv_rms = deep.tile([P, GT * NORMS], F32, name="inv_rms")
+            nc.scalar.activation(out=inv_rms[:], in_=sums[:], func=ACT.Abs_reciprocal_sqrt, bias=eps[:], scale=1.0 / D)
             state["y", g] = y_tiles
             state["inv_rms", g] = inv_rms
 

@@ -33,6 +33,8 @@ GT = 2
 XB = 4
 GROUPS_PER_CHUNK = T // GT
 N_GROUPS = N_CHUNKS * GROUPS_PER_CHUNK
+JOBS_PER_CHUNK = 4
+HEAD_JOBS = 6
 NORMS = 2 * HEADS
 
 FLOPS = 2 * (L_TXT + L_IMG) * DM * N_QKV
@@ -50,13 +52,6 @@ def load_weight(nc, consts, words_dram, scales_dram, label):
             in_=scales_dram[0, 4 * quadrant : 4 * quadrant + 4, :].bitcast(I32),
         )
     return words, plane
-
-
-def load_gains(nc, consts, q_gain, k_gain, label):
-    gain = consts.tile([P, 2, D], BF16, name=label + "_gain")
-    nc.scalar.dma_start(out=gain[:, 0, :], in_=q_gain.partition_broadcast(P))
-    nc.scalar.dma_start(out=gain[:, 1, :], in_=k_gain.partition_broadcast(P))
-    return gain
 
 
 def tile_fluxattention_pa_t_kernel(
@@ -86,6 +81,7 @@ def tile_fluxattention_pa_t_kernel(
         xt_psum = ctx.enter_context(tc.psum_pool(name="xt_psum", bufs=2))
         y_psum = ctx.enter_context(tc.psum_pool(name="y_psum", bufs=5))
         gain_psum = ctx.enter_context(tc.psum_pool(name="gain_psum", bufs=1))
+        scaled_pool = ctx.enter_context(tc.tile_pool(name="scaled", bufs=4))
         ctx.enter_context(tc.manual_schedule())
 
         def chunk_rows(c):
@@ -95,36 +91,44 @@ def tile_fluxattention_pa_t_kernel(
                 rows = hidden_states[0, (c - TXT_CHUNKS) * CHUNK : (c - TXT_CHUNKS + 1) * CHUNK, :]
             return rows.rearrange("(p t) k -> p t k", t=T)
 
+        gain_rows = consts.tile([P, 2, 2, D], BF16, name="gain_rows")
+        nc.vector.memset(gain_rows[:], 0.0)
+        ones = consts.tile([P, P], BF16, name="ones")
+        nc.vector.memset(ones[:], 1.0)
+        for s, stream_gains in enumerate(((eqn_scale, ekn_scale), (qn_scale, kn_scale))):
+            for qk, gain in enumerate(stream_gains):
+                nc.scalar.dma_start(out=gain_rows[0:1, s, qk, :], in_=gain.partition_broadcast(1))
+
         x_tiles = []
         table_tiles = []
         weights = {}
+
+        def load_table(c):
+            table = table_pool.tile([P, T, 2 * D], BF16, name="table")
+            nc.sync.dma_start(
+                out=table[:],
+                in_=image_rotary_emb[c * CHUNK : (c + 1) * CHUNK].rearrange("(p t) i f -> p t (i f)", t=T),
+            )
+            table_tiles.append(table)
+
         for c in range(N_CHUNKS):
             for part in range(T // XB):
                 x_sb = x_pool.tile([P, XB, DM], BF16, name="x_sb")
                 nc.sync.dma_start(out=x_sb[:], in_=chunk_rows(c)[:, part * XB : (part + 1) * XB, :])
                 x_tiles.append(x_sb)
                 if part == 0:
-                    table = table_pool.tile([P, T, 2 * D], BF16, name="table")
-                    nc.sync.dma_start(
-                        out=table[:],
-                        in_=image_rotary_emb[c * CHUNK : (c + 1) * CHUNK].rearrange("(p t) i f -> p t (i f)", t=T),
-                    )
-                    table_tiles.append(table)
                     if c == 0:
+                        load_table(0)
                         weights["txt"] = load_weight(nc, consts, W_eqkv_words, W_eqkv_scales, "txt")
+                    if c + 1 < N_CHUNKS:
+                        load_table(c + 1)
                     if c == 1:
                         weights["img"] = load_weight(nc, consts, W_iqkv_words, W_iqkv_scales, "img")
 
-        gains = {
-            "txt": load_gains(nc, consts, eqn_scale, ekn_scale, "txt"),
-            "img": load_gains(nc, consts, qn_scale, kn_scale, "img"),
-        }
         ident = consts.tile([P, P], F32, name="ident")
         make_identity(nc, ident[:])
-        ident_bf = consts.tile([P, P], BF16, name="ident_bf")
-        make_identity(nc, ident_bf[:])
         gains_ps = gain_psum.tile([P, 2, 2, D], F32, name="gains_ps")
-        STREAMS = ("txt", "img")
+        gains_sb = consts.tile([P, 2, 2, D], F32, name="gains_sb")
         eps = consts.tile([P, 1], F32, name="eps")
         nc.vector.memset(eps[:], EPS)
 
@@ -157,13 +161,13 @@ def tile_fluxattention_pa_t_kernel(
             state["codes", g] = codes
             state["x_plane", g] = x_plane
 
-        def scale_table(c, qk, a):
-            stream = "txt" if c < TXT_CHUNKS else "img"
+        def scale_table(engine, gains, job):
+            c, qk, a = job
             if qk == 0 and a == 0:
-                state["scaled", c] = deep.tile([P, T, 2, 2, D], F32, name="scaled")
-            nc.vector.tensor_tensor(
+                state["scaled", c] = scaled_pool.tile([P, T, 2, 2, D], F32, name="scaled")
+            engine.tensor_tensor(
                 out=state["scaled", c][:, :, qk, a, :].rearrange("p t (i b) -> p t i b", b=2),
-                in0=gains_ps[:, STREAMS.index(stream), qk, :]
+                in0=gains[:, int(c >= TXT_CHUNKS), qk, :]
                 .rearrange("p (o i b) -> p o i b", o=1, b=2)
                 .to_broadcast([P, T, D // 2, 2]),
                 in1=table_tiles[c][:].rearrange("p t (i a b) -> p t i a b", a=2, b=2)[:, :, :, a, :],
@@ -256,23 +260,31 @@ def tile_fluxattention_pa_t_kernel(
                 )
                 store(out, rotated[:, qk], g)
 
+        jobs = [(c, qk, a) for c in range(N_CHUNKS) for qk in range(2) for a in range(2)]
+        head_jobs = jobs[JOBS_PER_CHUNK : JOBS_PER_CHUNK + HEAD_JOBS]
+        later_jobs = jobs[JOBS_PER_CHUNK + HEAD_JOBS :]
+        spread = N_GROUPS - 2 * GROUPS_PER_CHUNK
+
         for step in range(N_GROUPS + 3):
-            c, quarter = divmod(step, GROUPS_PER_CHUNK)
             if step < N_GROUPS:
                 transpose_and_quantise(step)
             if step == 0:
-                for s, stream in enumerate(STREAMS):
-                    nc.tensor.matmul(
-                        out=gains_ps[:, s].rearrange("p q f -> p (q f)"),
-                        lhsT=ident_bf[:],
-                        rhs=gains[stream][:].rearrange("p q f -> p (q f)"),
-                        start=True,
-                        stop=True,
-                    )
-                for first_quarter in range(GROUPS_PER_CHUNK):
-                    scale_table(0, first_quarter // 2, first_quarter % 2)
-            if c + 1 < N_CHUNKS:
-                scale_table(c + 1, quarter // 2, quarter % 2)
+                nc.tensor.matmul(
+                    out=gains_ps[:].rearrange("p s q f -> p (s q f)"),
+                    lhsT=ones[:],
+                    rhs=gain_rows[:].rearrange("p s q f -> p (s q f)"),
+                    start=True,
+                    stop=True,
+                )
+                nc.scalar.copy(out=gains_sb[:], in_=gains_ps[:])
+                for job in jobs[:JOBS_PER_CHUNK]:
+                    scale_table(nc.vector, gains_ps, job)
+                for job in head_jobs:
+                    scale_table(nc.gpsimd, gains_sb, job)
+            turn = step - GROUPS_PER_CHUNK
+            if 0 <= turn < spread:
+                for job in later_jobs[turn * len(later_jobs) // spread : (turn + 1) * len(later_jobs) // spread]:
+                    scale_table(nc.vector, gains_ps, job)
             if 1 <= step < N_GROUPS + 1:
                 project(step - 1)
             if step >= 3:

@@ -41,17 +41,34 @@ FLOPS = 2 * (L_TXT + L_IMG) * DM * N_QKV
 
 
 def load_weight(nc, consts, words_dram, scales_dram, label):
+    raw_words = consts.tile([P, 2 * N_QK], U8, name=label + "_raw_words", align_bytes=64)
     words = consts.tile([P, 2 * N_PASS], U8, name=label + "_words", align_bytes=64)
-    nc.vector.memset(words[:, 2 * N_QKV :].bitcast(I32), 0)
-    nc.sync.dma_start(out=words[:, : 2 * N_QKV].bitcast(I32), in_=words_dram[0].bitcast(I32))
+    raw_plane = consts.tile([P, N_QKV], U8, name=label + "_raw_plane", align_bytes=64)
     plane = consts.tile([P, N_PASS], U8, name=label + "_plane", align_bytes=64)
-    nc.vector.memset(plane[:].bitcast(I32), 0)
+    nc.vector.memset(raw_plane[:].bitcast(I32), 0)
+    nc.vector.memset(words[:, 2 * N_QKV :].bitcast(I32), 0)
+    nc.vector.memset(plane[:, N_QKV:].bitcast(I32), 0)
+    nc.sync.dma_start(out=raw_words[:].bitcast(I32), in_=words_dram[0, :, : 2 * N_QK].bitcast(I32))
     for quadrant in range(4):
         nc.sync.dma_start(
-            out=plane[32 * quadrant : 32 * quadrant + 4, :N_QKV].bitcast(I32),
+            out=raw_plane[32 * quadrant : 32 * quadrant + 4, :].bitcast(I32),
             in_=scales_dram[0, 4 * quadrant : 4 * quadrant + 4, :].bitcast(I32),
         )
-    return words, plane
+    nc.sync.dma_start(out=words[:, 2 * N_QK : 2 * N_QKV].bitcast(I32), in_=words_dram[0, :, 2 * N_QK :].bitcast(I32))
+    return raw_words, raw_plane, words, plane
+
+
+def sort_columns(nc, weight):
+    raw_words, raw_plane, words, plane = weight
+    source = raw_words[:].rearrange("p (n i b y) -> p n i b y", n=NORMS, b=2, y=2)
+    target = words[:, : 2 * N_QK].rearrange("p (n b i y) -> p n b i y", n=NORMS, b=2, y=2)
+    for b in range(2):
+        nc.vector.tensor_copy(out=target[:, :, b], in_=source[:, :, :, b])
+    nc.vector.tensor_copy(
+        out=plane[:, :N_QK].rearrange("p (n b i) -> p n b i", n=NORMS, b=2),
+        in_=raw_plane[:, :N_QK].rearrange("p (n i b) -> p n b i", n=NORMS, b=2),
+    )
+    nc.vector.tensor_copy(out=plane[:, N_QK:N_QKV], in_=raw_plane[:, N_QK:])
 
 
 def tile_fluxattention_pa_t_kernel(
@@ -118,8 +135,8 @@ def tile_fluxattention_pa_t_kernel(
                 x_tiles.append(x_sb)
                 if part == 0:
                     if c == 0:
-                        load_table(0)
                         weights["txt"] = load_weight(nc, consts, W_eqkv_words, W_eqkv_scales, "txt")
+                        load_table(0)
                     if c + 1 < N_CHUNKS:
                         load_table(c + 1)
                     if c == 1:
@@ -131,6 +148,8 @@ def tile_fluxattention_pa_t_kernel(
         gains_sb = consts.tile([P, 2, 2, D], F32, name="gains_sb")
         eps = consts.tile([P, 1], F32, name="eps")
         nc.vector.memset(eps[:], EPS)
+        first = consts.tile([P, 1], F32, name="first")
+        nc.scalar.activation(out=first[:], in_=eps[:], func=ACT.Abs_reciprocal_sqrt, bias=eps[:], scale=1.0 / D)
 
         state = {}
 
@@ -162,15 +181,16 @@ def tile_fluxattention_pa_t_kernel(
             state["x_plane", g] = x_plane
 
         def scale_table(engine, gains, job):
-            c, qk, a = job
-            if qk == 0 and a == 0:
-                state["scaled", c] = scaled_pool.tile([P, T, 2, 2, D], F32, name="scaled")
+            c, qk, half = job
+            if qk == 0 and half == 0:
+                state["scaled", c] = scaled_pool.tile([P, T, 2, 2 * D], F32, name="scaled")
+            tokens = slice(half * (T // 2), (half + 1) * (T // 2))
             engine.tensor_tensor(
-                out=state["scaled", c][:, :, qk, a, :].rearrange("p t (i b) -> p t i b", b=2),
+                out=state["scaled", c][:, tokens, qk, :].rearrange("p t (b i a) -> p t b i a", b=2, a=2),
                 in0=gains[:, int(c >= TXT_CHUNKS), qk, :]
-                .rearrange("p (o i b) -> p o i b", o=1, b=2)
-                .to_broadcast([P, T, D // 2, 2]),
-                in1=table_tiles[c][:].rearrange("p t (i a b) -> p t i a b", a=2, b=2)[:, :, :, a, :],
+                .rearrange("p (o b i z) -> p o b i z", o=1, b=2, z=1)
+                .to_broadcast([P, T // 2, 2, D // 2, 2]),
+                in1=table_tiles[c][:, tokens, :].rearrange("p t (i a b) -> p t b i a", a=2, b=2),
                 op=ALU.mult,
             )
 
@@ -186,7 +206,7 @@ def tile_fluxattention_pa_t_kernel(
         def project(g):
             codes = state["codes", g]
             x_plane = state["x_plane", g]
-            w_words, w_plane = weights[stream_of(g)]
+            w_words, w_plane = weights[stream_of(g)][2:]
             c, half = divmod(g, GROUPS_PER_CHUNK)
             y_tiles = []
             for j in range(GT):
@@ -227,16 +247,16 @@ def tile_fluxattention_pa_t_kernel(
             inv_rms = state["inv_rms", g]
             c, half = divmod(g, GROUPS_PER_CHUNK)
             scaled = state["scaled", c]
-            terms = work.tile([P, 2, GT, HEADS, 2, D], F32, name="terms")
+            terms = work.tile([P, 2, GT, HEADS, 2 * D], F32, name="terms")
             for j in range(GT):
                 for n in range(NORMS):
                     qk, head = divmod(n, HEADS)
-                    y = y_tiles[j][:, n * D : (n + 1) * D].rearrange("p (o f) -> p o f", o=1)
+                    y = y_tiles[j][:, n * D : (n + 1) * D].rearrange("p (f o) -> p f o", o=1)
                     nc.vector.scalar_tensor_tensor(
-                        out=terms[:, qk, j, head],
-                        in0=y.to_broadcast([P, 2, D]),
+                        out=terms[:, qk, j, head].rearrange("p (f a) -> p f a", a=2),
+                        in0=y.to_broadcast([P, D, 2]),
                         scalar=inv_rms[:, j * NORMS + n : j * NORMS + n + 1],
-                        in1=scaled[:, half * GT + j, qk],
+                        in1=scaled[:, half * GT + j, qk].rearrange("p (f a) -> p f a", a=2),
                         op0=ALU.mult,
                         op1=ALU.mult,
                     )
@@ -249,38 +269,47 @@ def tile_fluxattention_pa_t_kernel(
                 state["rotated", c] = deep.tile([P, 2, T, HD], F32, name="rotated")
             rotated = state["rotated", c]
             blocks = slice(half * GT, (half + 1) * GT)
-            engine = nc.vector if g == N_GROUPS - 1 else nc.gpsimd
-            for qk, out in enumerate((out_0, out_1)):
-                pairs = terms[:, qk].rearrange("p j h a (i b) -> p (j h) i a b", b=2)
+            if g == N_GROUPS - 1:
+                engine, parts = nc.vector, (slice(0, 1), slice(1, 2))
+            else:
+                engine, parts = nc.gpsimd, (slice(0, 2),)
+            for part in parts:
+                both = terms[:, part].rearrange("p q j h (b f) -> p q (j h) b f", b=2)
                 engine.tensor_tensor(
-                    out=rotated[:, qk, blocks, :].rearrange("p j (h i a) -> p (j h) i a", h=HEADS, a=2),
-                    in0=pairs[:, :, :, :, 0],
-                    in1=pairs[:, :, :, :, 1],
+                    out=rotated[:, part, blocks, :].rearrange("p q j (h f) -> p q (j h) f", h=HEADS),
+                    in0=both[:, :, :, 0],
+                    in1=both[:, :, :, 1],
                     op=ALU.add,
                 )
-                store(out, rotated[:, qk], g)
+                for qk, out in list(enumerate((out_0, out_1)))[part]:
+                    store(out, rotated[:, qk], g)
 
-        jobs = [(c, qk, a) for c in range(N_CHUNKS) for qk in range(2) for a in range(2)]
+        jobs = [(c, qk, half) for c in range(N_CHUNKS) for qk in range(2) for half in range(2)]
         head_jobs = jobs[JOBS_PER_CHUNK : JOBS_PER_CHUNK + HEAD_JOBS]
         later_jobs = jobs[JOBS_PER_CHUNK + HEAD_JOBS :]
         spread = N_GROUPS - 2 * GROUPS_PER_CHUNK
 
+        sort_columns(nc, weights["txt"])
         for step in range(N_GROUPS + 3):
             if step < N_GROUPS:
                 transpose_and_quantise(step)
             if step == 0:
-                nc.tensor.matmul(
-                    out=gains_ps[:].rearrange("p s q f -> p (s q f)"),
-                    lhsT=ones[:],
-                    rhs=gain_rows[:].rearrange("p s q f -> p (s q f)"),
-                    start=True,
-                    stop=True,
-                )
+                for s in range(2):
+                    for qk in range(2):
+                        nc.tensor.matmul(
+                            out=gains_ps[:, s, qk, :],
+                            lhsT=ones[:],
+                            rhs=gain_rows[:, s, qk, :].rearrange("p (i b) -> p b i", b=2),
+                            start=True,
+                            stop=True,
+                        )
                 nc.scalar.copy(out=gains_sb[:], in_=gains_ps[:])
                 for job in jobs[:JOBS_PER_CHUNK]:
                     scale_table(nc.vector, gains_ps, job)
                 for job in head_jobs:
                     scale_table(nc.gpsimd, gains_sb, job)
+            if step == GROUPS_PER_CHUNK:
+                sort_columns(nc, weights["img"])
             turn = step - GROUPS_PER_CHUNK
             if 0 <= turn < spread:
                 for job in later_jobs[turn * len(later_jobs) // spread : (turn + 1) * len(later_jobs) // spread]:

@@ -22,19 +22,17 @@ D = 64
 HD = HEADS * D
 N_QK = 2 * HD
 N_QKV = 3 * HD
-N_PASS = 512
 EPS = 1e-6
 
 T = 8
 CHUNK = P * T
 N_CHUNKS = (L_TXT + L_IMG) // CHUNK
 TXT_CHUNKS = L_TXT // CHUNK
-GT = 2
-XB = 4
-GROUPS_PER_CHUNK = T // GT
-N_GROUPS = N_CHUNKS * GROUPS_PER_CHUNK
+PAIR = 2
+GROUP = 4
 JOBS_PER_CHUNK = 4
 HEAD_JOBS = 6
+GPSIMD_TURN = 3
 NORMS = 2 * HEADS
 
 FLOPS = 2 * (L_TXT + L_IMG) * DM * N_QKV
@@ -42,12 +40,10 @@ FLOPS = 2 * (L_TXT + L_IMG) * DM * N_QKV
 
 def load_weight(nc, consts, words_dram, scales_dram, label):
     raw_words = consts.tile([P, 2 * N_QK], U8, name=label + "_raw_words", align_bytes=64)
-    words = consts.tile([P, 2 * N_PASS], U8, name=label + "_words", align_bytes=64)
+    words = consts.tile([P, 2 * N_QKV], U8, name=label + "_words", align_bytes=64)
     raw_plane = consts.tile([P, N_QKV], U8, name=label + "_raw_plane", align_bytes=64)
-    plane = consts.tile([P, N_PASS], U8, name=label + "_plane", align_bytes=64)
+    plane = consts.tile([P, N_QKV], U8, name=label + "_plane", align_bytes=64)
     nc.vector.memset(raw_plane[:].bitcast(I32), 0)
-    nc.vector.memset(words[:, 2 * N_QKV :].bitcast(I32), 0)
-    nc.vector.memset(plane[:, N_QKV:].bitcast(I32), 0)
     nc.sync.dma_start(out=raw_words[:].bitcast(I32), in_=words_dram[0, :, : 2 * N_QK].bitcast(I32))
     for quadrant in range(4):
         nc.sync.dma_start(
@@ -91,22 +87,26 @@ def tile_fluxattention_pa_t_kernel(
     nc = tc.nc
     with ExitStack() as ctx:
         consts = ctx.enter_context(tc.tile_pool(name="consts", bufs=1))
-        x_pool = ctx.enter_context(tc.tile_pool(name="x", bufs=N_CHUNKS * T // XB))
-        table_pool = ctx.enter_context(tc.tile_pool(name="table", bufs=N_CHUNKS))
         work = ctx.enter_context(tc.tile_pool(name="work", bufs=3))
         deep = ctx.enter_context(tc.tile_pool(name="deep", bufs=3))
+        scaled_pool = ctx.enter_context(tc.tile_pool(name="scaled", bufs=5))
         xt_psum = ctx.enter_context(tc.psum_pool(name="xt_psum", bufs=2))
-        y_psum = ctx.enter_context(tc.psum_pool(name="y_psum", bufs=5))
+        qk_psum = ctx.enter_context(tc.psum_pool(name="qk_psum", bufs=4))
+        v_psum = ctx.enter_context(tc.psum_pool(name="v_psum", bufs=1))
         gain_psum = ctx.enter_context(tc.psum_pool(name="gain_psum", bufs=1))
-        scaled_pool = ctx.enter_context(tc.tile_pool(name="scaled", bufs=4))
         ctx.enter_context(tc.manual_schedule())
 
-        def chunk_rows(c):
-            if c < TXT_CHUNKS:
-                rows = encoder_hidden_states[0, c * CHUNK : (c + 1) * CHUNK, :]
-            else:
-                rows = hidden_states[0, (c - TXT_CHUNKS) * CHUNK : (c - TXT_CHUNKS + 1) * CHUNK, :]
-            return rows.rearrange("(p t) k -> p t k", t=T)
+        groups = []
+        for c in range(N_CHUNKS):
+            sizes = [GROUP] * (T // GROUP)
+            if c == 0:
+                sizes = [PAIR, PAIR] + sizes[1:]
+            if c == N_CHUNKS - 1:
+                sizes = sizes[1:] + [PAIR, PAIR]
+            first = 0
+            for size in sizes:
+                groups.append((c, first, size))
+                first += size
 
         gain_rows = consts.tile([P, 2, 2, D], BF16, name="gain_rows")
         nc.vector.memset(gain_rows[:], 0.0)
@@ -116,31 +116,40 @@ def tile_fluxattention_pa_t_kernel(
             for qk, gain in enumerate(stream_gains):
                 nc.scalar.dma_start(out=gain_rows[0:1, s, qk, :], in_=gain.partition_broadcast(1))
 
-        x_tiles = []
+        x_blocks = []
         table_tiles = []
         weights = {}
 
+        def load_x(c, first, size):
+            if c < TXT_CHUNKS:
+                rows = encoder_hidden_states[0, c * CHUNK : (c + 1) * CHUNK, :]
+            else:
+                rows = hidden_states[0, (c - TXT_CHUNKS) * CHUNK : (c - TXT_CHUNKS + 1) * CHUNK, :]
+            x_sb = consts.tile([P, size, DM], BF16, name="x_%d_%d" % (c, first))
+            nc.sync.dma_start(out=x_sb[:], in_=rows.rearrange("(p t) k -> p t k", t=T)[:, first : first + size, :])
+            x_blocks.extend((x_sb, j) for j in range(size))
+
         def load_table(c):
-            table = table_pool.tile([P, T, 2 * D], BF16, name="table")
+            table = consts.tile([P, T, 2 * D], BF16, name="table_%d" % c)
             nc.sync.dma_start(
                 out=table[:],
                 in_=image_rotary_emb[c * CHUNK : (c + 1) * CHUNK].rearrange("(p t) i f -> p t (i f)", t=T),
             )
             table_tiles.append(table)
 
-        for c in range(N_CHUNKS):
-            for part in range(T // XB):
-                x_sb = x_pool.tile([P, XB, DM], BF16, name="x_sb")
-                nc.sync.dma_start(out=x_sb[:], in_=chunk_rows(c)[:, part * XB : (part + 1) * XB, :])
-                x_tiles.append(x_sb)
-                if part == 0:
-                    if c == 0:
-                        weights["txt"] = load_weight(nc, consts, W_eqkv_words, W_eqkv_scales, "txt")
-                        load_table(0)
-                    if c + 1 < N_CHUNKS:
-                        load_table(c + 1)
-                    if c == 1:
-                        weights["img"] = load_weight(nc, consts, W_iqkv_words, W_iqkv_scales, "img")
+        load_x(0, 0, PAIR)
+        weights["txt"] = load_weight(nc, consts, W_eqkv_words, W_eqkv_scales, "txt")
+        load_x(0, PAIR, PAIR)
+        load_table(0)
+        load_x(0, GROUP, GROUP)
+        load_table(1)
+        for c in range(1, N_CHUNKS):
+            for first in range(0, T, GROUP):
+                load_x(c, first, GROUP)
+            if c + 1 < N_CHUNKS:
+                load_table(c + 1)
+            if c == 1:
+                weights["img"] = load_weight(nc, consts, W_iqkv_words, W_iqkv_scales, "img")
 
         ident = consts.tile([P, P], F32, name="ident")
         make_identity(nc, ident[:])
@@ -148,41 +157,41 @@ def tile_fluxattention_pa_t_kernel(
         gains_sb = consts.tile([P, 2, 2, D], F32, name="gains_sb")
         eps = consts.tile([P, 1], F32, name="eps")
         nc.vector.memset(eps[:], EPS)
-        first = consts.tile([P, 1], F32, name="first")
-        nc.scalar.activation(out=first[:], in_=eps[:], func=ACT.Abs_reciprocal_sqrt, bias=eps[:], scale=1.0 / D)
+        first_root = consts.tile([P, 1], F32, name="first_root")
+        nc.scalar.activation(out=first_root[:], in_=eps[:], func=ACT.Abs_reciprocal_sqrt, bias=eps[:], scale=1.0 / D)
 
         state = {}
 
-        def stream_of(g):
-            return "txt" if g // GROUPS_PER_CHUNK < TXT_CHUNKS else "img"
-
-        def transpose_and_quantise(g):
-            load, first = divmod(g * GT, XB)
-            x_words = x_tiles[load][:].bitcast(F32)
-            grouped = work.tile([P, GT, P, 4], BF16, name="grouped", align_bytes=64)
-            grouped_words = grouped[:].bitcast(F32)
-            for pair in range(GT // 2):
-                xt = xt_psum.tile([P, 2, 2, P], F32, name="xt")
-                for j in range(2):
+        def transpose(g):
+            c, first, size = groups[g]
+            grouped = work.tile([P, GROUP, P, 4], BF16, name="grouped", align_bytes=64)
+            for pair in range(size // PAIR):
+                xt = xt_psum.tile([P, PAIR, 2, P], F32, name="xt")
+                for j in range(PAIR):
+                    x_sb, place = x_blocks[c * T + first + PAIR * pair + j]
+                    x_words = x_sb[:, place, :].bitcast(F32)
                     for u in range(2):
-                        nc.tensor.transpose(xt[:, j, u, :], x_words[:, first + 2 * pair + j, u : DM // 2 : 2], ident[:])
+                        nc.tensor.transpose(xt[:, j, u, :], x_words[:, u : DM // 2 : 2], ident[:])
                 nc.scalar.copy(
-                    out=grouped_words[:, 2 * pair : 2 * pair + 2, :, :],
+                    out=grouped[:, PAIR * pair : PAIR * (pair + 1), :, :].bitcast(F32),
                     in_=xt[:].rearrange("p j u r -> p j r u"),
                 )
-            codes = work.tile([P, GT * P], U32, name="codes", align_bytes=64)
-            x_plane = work.tile([P, GT * P], U8, name="x_plane", align_bytes=64)
+            state["grouped", g] = grouped
+
+        def quantise(g):
+            size = groups[g][2]
+            codes = work.tile([P, GROUP * P], U32, name="codes", align_bytes=64)
+            x_plane = work.tile([P, GROUP * P], U8, name="x_plane", align_bytes=64)
             nc.vector.quantize_mx(
-                out=codes[:].bitcast(FP8X4),
-                scales=x_plane[:],
-                in_=grouped[:].rearrange("p j r t -> p (j r t)"),
+                out=codes[:, : size * P].bitcast(FP8X4),
+                scales=x_plane[:, : size * P],
+                in_=state["grouped", g][:, :size].rearrange("p j r t -> p (j r t)"),
             )
-            state["codes", g] = codes
-            state["x_plane", g] = x_plane
+            state["codes", g] = codes, x_plane
 
         def scale_table(engine, gains, job):
-            c, qk, half = job
-            if qk == 0 and half == 0:
+            c, half, qk = job
+            if half == 0 and qk == 0:
                 state["scaled", c] = scaled_pool.tile([P, T, 2, 2 * D], F32, name="scaled")
             tokens = slice(half * (T // 2), (half + 1) * (T // 2))
             engine.tensor_tensor(
@@ -195,128 +204,162 @@ def tile_fluxattention_pa_t_kernel(
             )
 
         def store(out, tile, g):
-            c, half = divmod(g, GROUPS_PER_CHUNK)
+            c, first, size = groups[g]
             rows = out[0, c * CHUNK : (c + 1) * CHUNK, :].rearrange("(p t) f -> p t f", t=T)
             if c == N_CHUNKS - 1:
-                blocks = slice(half * GT, (half + 1) * GT)
+                blocks = slice(first, first + size)
                 nc.sync.dma_start(out=rows[:, blocks, :], in_=tile[:, blocks, :])
-            elif half == GROUPS_PER_CHUNK - 1:
+            elif first + size == T:
                 nc.sync.dma_start(out=rows, in_=tile[:])
 
         def project(g):
-            codes = state["codes", g]
-            x_plane = state["x_plane", g]
-            w_words, w_plane = weights[stream_of(g)][2:]
-            c, half = divmod(g, GROUPS_PER_CHUNK)
-            y_tiles = []
-            for j in range(GT):
-                y_ps = y_psum.tile([P, N_PASS], F32, name="y_ps")
-                y_tiles.append(y_ps)
+            c, first, size = groups[g]
+            codes, x_plane = state["codes", g]
+            w_words, w_plane = weights["txt" if c < TXT_CHUNKS else "img"][2:]
+
+            def one_pass(out, j, columns):
                 nc.tensor.matmul_mx(
-                    out=y_ps[:],
+                    out=out,
                     lhsT=codes[:, j * P : (j + 1) * P].bitcast(FP8X4),
                     lhsT_scale=x_plane[:, j * P : (j + 1) * P],
-                    rhs=w_words[:].bitcast(FP4X4),
-                    rhs_scale=w_plane[:],
+                    rhs=w_words[:, 2 * columns.start : 2 * columns.stop].bitcast(FP4X4),
+                    rhs_scale=w_plane[:, columns],
                     start=True,
                     stop=True,
                 )
-            squares = work.tile([P, GT, NORMS, D], BF16, name="squares")
-            sums = deep.tile([P, GT * NORMS], F32, name="sums")
-            for j in range(GT):
+
+            qk_tiles = []
+            for pair in range(size // PAIR):
+                qk_ps = qk_psum.tile([P, PAIR, N_QK], F32, name="qk_ps")
+                qk_tiles.append(qk_ps)
+                for j in range(PAIR):
+                    one_pass(qk_ps[:, j, :], PAIR * pair + j, slice(0, N_QK))
+            v_ps = v_psum.tile([P, GROUP, HD], F32, name="v_ps")
+            for j in range(size):
+                one_pass(v_ps[:, j, :], j, slice(N_QK, N_QKV))
+            state["y", g] = qk_tiles, v_ps
+
+        def square(g):
+            c, first, size = groups[g]
+            qk_tiles = state["y", g][0]
+            squares = work.tile([P, NORMS, D], BF16, name="squares")
+            sums = deep.tile([P, GROUP * NORMS], F32, name="sums")
+            for j in range(size):
                 for n in range(NORMS):
                     nc.scalar.activation(
-                        out=squares[:, j, n, :],
-                        in_=y_tiles[j][:, n * D : (n + 1) * D],
+                        out=squares[:, n, :],
+                        in_=qk_tiles[j // PAIR][:, j % PAIR, n * D : (n + 1) * D],
                         func=ACT.Square,
                         accum_out=sums[:, j * NORMS + n : j * NORMS + n + 1],
                     )
-            if half == 0:
+            state["sums", g] = sums
+
+        def finish_norms(g):
+            c, first, size = groups[g]
+            v_ps = state["y", g][1]
+            sums = state["sums", g]
+            if first == 0:
                 state["v_sb", c] = deep.tile([P, T, HD], F32, name="v_sb")
             v_sb = state["v_sb", c]
-            for j in range(GT):
-                nc.scalar.copy(out=v_sb[:, half * GT + j, :], in_=y_tiles[j][:, N_QK:N_QKV])
+            nc.scalar.copy(out=v_sb[:, first : first + size, :], in_=v_ps[:, :size, :])
             store(out_2, v_sb, g)
-            inv_rms = deep.tile([P, GT * NORMS], F32, name="inv_rms")
-            nc.scalar.activation(out=inv_rms[:], in_=sums[:], func=ACT.Abs_reciprocal_sqrt, bias=eps[:], scale=1.0 / D)
-            state["y", g] = y_tiles
+            inv_rms = deep.tile([P, GROUP * NORMS], F32, name="inv_rms")
+            nc.scalar.activation(
+                out=inv_rms[:, : size * NORMS],
+                in_=sums[:, : size * NORMS],
+                func=ACT.Abs_reciprocal_sqrt,
+                bias=eps[:],
+                scale=1.0 / D,
+            )
             state["inv_rms", g] = inv_rms
 
         def multiply(g):
-            y_tiles = state["y", g]
+            c, first, size = groups[g]
+            qk_tiles = state["y", g][0]
             inv_rms = state["inv_rms", g]
-            c, half = divmod(g, GROUPS_PER_CHUNK)
             scaled = state["scaled", c]
-            terms = work.tile([P, 2, GT, HEADS, 2 * D], F32, name="terms")
-            for j in range(GT):
+            terms = work.tile([P, 2, GROUP, HEADS, 2 * D], F32, name="terms")
+            for j in range(size):
                 for n in range(NORMS):
                     qk, head = divmod(n, HEADS)
-                    y = y_tiles[j][:, n * D : (n + 1) * D].rearrange("p (f o) -> p f o", o=1)
+                    y = qk_tiles[j // PAIR][:, j % PAIR, n * D : (n + 1) * D].rearrange("p (f o) -> p f o", o=1)
                     nc.vector.scalar_tensor_tensor(
                         out=terms[:, qk, j, head].rearrange("p (f a) -> p f a", a=2),
                         in0=y.to_broadcast([P, D, 2]),
                         scalar=inv_rms[:, j * NORMS + n : j * NORMS + n + 1],
-                        in1=scaled[:, half * GT + j, qk].rearrange("p (f a) -> p f a", a=2),
+                        in1=scaled[:, first + j, qk].rearrange("p (f a) -> p f a", a=2),
                         op0=ALU.mult,
                         op1=ALU.mult,
                     )
             state["terms", g] = terms
 
         def add_terms(g):
+            c, first, size = groups[g]
             terms = state["terms", g]
-            c, half = divmod(g, GROUPS_PER_CHUNK)
-            if half == 0:
+            if first == 0:
                 state["rotated", c] = deep.tile([P, 2, T, HD], F32, name="rotated")
             rotated = state["rotated", c]
-            blocks = slice(half * GT, (half + 1) * GT)
-            if g == N_GROUPS - 1:
-                engine, parts = nc.vector, (slice(0, 1), slice(1, 2))
-            else:
-                engine, parts = nc.gpsimd, (slice(0, 2),)
-            for part in parts:
-                both = terms[:, part].rearrange("p q j h (b f) -> p q (j h) b f", b=2)
+            engine = nc.vector if g == len(groups) - 1 else nc.gpsimd
+            for qk, out in enumerate((out_0, out_1)):
+                both = terms[:, qk, :size].rearrange("p j h (b f) -> p (j h) b f", b=2)
                 engine.tensor_tensor(
-                    out=rotated[:, part, blocks, :].rearrange("p q j (h f) -> p q (j h) f", h=HEADS),
-                    in0=both[:, :, :, 0],
-                    in1=both[:, :, :, 1],
+                    out=rotated[:, qk, first : first + size, :].rearrange("p j (h f) -> p (j h) f", h=HEADS),
+                    in0=both[:, :, 0],
+                    in1=both[:, :, 1],
                     op=ALU.add,
                 )
-                for qk, out in list(enumerate((out_0, out_1)))[part]:
-                    store(out, rotated[:, qk], g)
+                store(out, rotated[:, qk], g)
 
-        jobs = [(c, qk, half) for c in range(N_CHUNKS) for qk in range(2) for half in range(2)]
+        jobs = [(c, half, qk) for c in range(N_CHUNKS) for half in range(2) for qk in range(2)]
         head_jobs = jobs[JOBS_PER_CHUNK : JOBS_PER_CHUNK + HEAD_JOBS]
         later_jobs = jobs[JOBS_PER_CHUNK + HEAD_JOBS :]
-        spread = N_GROUPS - 2 * GROUPS_PER_CHUNK
+        first_turn = 3
+        turns = len(groups) - first_turn - 2
+
+        def turn_jobs(step, gpsimd):
+            turn = step - first_turn
+            if not 0 <= turn < turns:
+                return []
+            numbers = range(turn * len(later_jobs) // turns, (turn + 1) * len(later_jobs) // turns)
+            return [later_jobs[n] for n in numbers if (n % GPSIMD_TURN == GPSIMD_TURN - 1) == gpsimd]
 
         sort_columns(nc, weights["txt"])
-        for step in range(N_GROUPS + 3):
-            if step < N_GROUPS:
-                transpose_and_quantise(step)
+        transpose(0)
+        for s in range(2):
+            for qk in range(2):
+                nc.tensor.matmul(
+                    out=gains_ps[:, s, qk, :],
+                    lhsT=ones[:],
+                    rhs=gain_rows[:, s, qk, :].rearrange("p (i b) -> p b i", b=2),
+                    start=True,
+                    stop=True,
+                )
+        for step in range(len(groups) + 3):
+            if step + 1 < len(groups) and step != 1:
+                transpose(step + 1)
+            if 1 <= step < len(groups) + 1:
+                project(step - 1)
+                square(step - 1)
+            if step == 1:
+                transpose(step + 1)
+            if 1 <= step < len(groups) + 1:
+                finish_norms(step - 1)
+            if step < len(groups):
+                quantise(step)
             if step == 0:
-                for s in range(2):
-                    for qk in range(2):
-                        nc.tensor.matmul(
-                            out=gains_ps[:, s, qk, :],
-                            lhsT=ones[:],
-                            rhs=gain_rows[:, s, qk, :].rearrange("p (i b) -> p b i", b=2),
-                            start=True,
-                            stop=True,
-                        )
-                nc.scalar.copy(out=gains_sb[:], in_=gains_ps[:])
-                for job in jobs[:JOBS_PER_CHUNK]:
-                    scale_table(nc.vector, gains_ps, job)
+                nc.vector.tensor_copy(out=gains_sb[:], in_=gains_ps[:])
                 for job in head_jobs:
                     scale_table(nc.gpsimd, gains_sb, job)
-            if step == GROUPS_PER_CHUNK:
+            if step < 2:
+                for qk in range(2):
+                    scale_table(nc.vector, gains_ps, (0, step, qk))
+            if step == first_turn:
                 sort_columns(nc, weights["img"])
-            turn = step - GROUPS_PER_CHUNK
-            if 0 <= turn < spread:
-                for job in later_jobs[turn * len(later_jobs) // spread : (turn + 1) * len(later_jobs) // spread]:
-                    scale_table(nc.vector, gains_ps, job)
-            if 1 <= step < N_GROUPS + 1:
-                project(step - 1)
+            for job in turn_jobs(step, False):
+                scale_table(nc.vector, gains_ps, job)
             if step >= 3:
                 add_terms(step - 3)
-            if 2 <= step < N_GROUPS + 2:
+            for job in turn_jobs(step, True):
+                scale_table(nc.gpsimd, gains_sb, job)
+            if 2 <= step < len(groups) + 2:
                 multiply(step - 2)

@@ -30,8 +30,8 @@ N_CHUNKS = (L_TXT + L_IMG) // CHUNK
 TXT_CHUNKS = L_TXT // CHUNK
 PAIR = 2
 GROUP = 4
-JOBS_PER_CHUNK = 4
-HEAD_JOBS = 6
+HEAD_JOBS_VECTOR = 2
+HEAD_JOBS_GPSIMD = 6
 GPSIMD_TURN = 3
 NORMS = 2 * HEADS
 
@@ -141,8 +141,8 @@ def tile_fluxattention_pa_t_kernel(
         weights["txt"] = load_weight(nc, consts, W_eqkv_words, W_eqkv_scales, "txt")
         load_x(0, PAIR, PAIR)
         load_table(0)
-        load_x(0, GROUP, GROUP)
         load_table(1)
+        load_x(0, GROUP, GROUP)
         for c in range(1, N_CHUNKS):
             for first in range(0, T, GROUP):
                 load_x(c, first, GROUP)
@@ -191,7 +191,7 @@ def tile_fluxattention_pa_t_kernel(
 
         def scale_table(engine, gains, job):
             c, half, qk = job
-            if half == 0 and qk == 0:
+            if ("scaled", c) not in state:
                 state["scaled", c] = scaled_pool.tile([P, T, 2, 2 * D], F32, name="scaled")
             tokens = slice(half * (T // 2), (half + 1) * (T // 2))
             engine.tensor_tensor(
@@ -299,20 +299,23 @@ def tile_fluxattention_pa_t_kernel(
             if first == 0:
                 state["rotated", c] = deep.tile([P, 2, T, HD], F32, name="rotated")
             rotated = state["rotated", c]
-            engine = nc.vector if g == len(groups) - 1 else nc.gpsimd
-            for qk, out in enumerate((out_0, out_1)):
-                both = terms[:, qk, :size].rearrange("p j h (b f) -> p (j h) b f", b=2)
+            if g == len(groups) - 1:
+                engine, parts = nc.vector, (slice(0, 1), slice(1, 2))
+            else:
+                engine, parts = nc.gpsimd, (slice(0, 2),)
+            for part in parts:
+                both = terms[:, part, :size].rearrange("p q j h (b f) -> p q (j h) b f", b=2)
                 engine.tensor_tensor(
-                    out=rotated[:, qk, first : first + size, :].rearrange("p j (h f) -> p (j h) f", h=HEADS),
-                    in0=both[:, :, 0],
-                    in1=both[:, :, 1],
+                    out=rotated[:, part, first : first + size, :].rearrange("p q j (h f) -> p q (j h) f", h=HEADS),
+                    in0=both[:, :, :, 0],
+                    in1=both[:, :, :, 1],
                     op=ALU.add,
                 )
-                store(out, rotated[:, qk], g)
+                for qk in range(part.start, part.stop):
+                    store((out_0, out_1)[qk], rotated[:, qk], g)
 
         jobs = [(c, half, qk) for c in range(N_CHUNKS) for half in range(2) for qk in range(2)]
-        head_jobs = jobs[JOBS_PER_CHUNK : JOBS_PER_CHUNK + HEAD_JOBS]
-        later_jobs = jobs[JOBS_PER_CHUNK + HEAD_JOBS :]
+        later_jobs = jobs[HEAD_JOBS_VECTOR + HEAD_JOBS_GPSIMD :]
         first_turn = 3
         turns = len(groups) - first_turn - 2
 
@@ -348,11 +351,10 @@ def tile_fluxattention_pa_t_kernel(
                 quantise(step)
             if step == 0:
                 nc.vector.tensor_copy(out=gains_sb[:], in_=gains_ps[:])
-                for job in head_jobs:
+                for job in jobs[:HEAD_JOBS_VECTOR]:
+                    scale_table(nc.vector, gains_ps, job)
+                for job in jobs[HEAD_JOBS_VECTOR : HEAD_JOBS_VECTOR + HEAD_JOBS_GPSIMD]:
                     scale_table(nc.gpsimd, gains_sb, job)
-            if step < 2:
-                for qk in range(2):
-                    scale_table(nc.vector, gains_ps, (0, step, qk))
             if step == first_turn:
                 sort_columns(nc, weights["img"])
             for job in turn_jobs(step, False):

@@ -30,7 +30,7 @@ N_CHUNKS = (L_TXT + L_IMG) // CHUNK
 TXT_CHUNKS = L_TXT // CHUNK
 PAIR = 2
 GROUP = 4
-HEAD_JOBS_VECTOR = 2
+HEAD_JOBS_VECTOR = 4
 HEAD_JOBS_GPSIMD = 6
 GPSIMD_TURN = 3
 NORMS = 2 * HEADS
@@ -39,32 +39,36 @@ FLOPS = 2 * (L_TXT + L_IMG) * DM * N_QKV
 
 
 def load_weight(nc, consts, words_dram, scales_dram, label):
-    raw_words = consts.tile([P, 2 * N_QK], U8, name=label + "_raw_words", align_bytes=64)
+    raw_words = consts.tile([P, 2 * N_QKV], U8, name=label + "_raw_words", align_bytes=64)
     words = consts.tile([P, 2 * N_QKV], U8, name=label + "_words", align_bytes=64)
     raw_plane = consts.tile([P, N_QKV], U8, name=label + "_raw_plane", align_bytes=64)
     plane = consts.tile([P, N_QKV], U8, name=label + "_plane", align_bytes=64)
+    nc.sync.dma_start(out=raw_words[:].bitcast(I32), in_=words_dram[0].bitcast(I32))
     nc.vector.memset(raw_plane[:].bitcast(I32), 0)
-    nc.sync.dma_start(out=raw_words[:].bitcast(I32), in_=words_dram[0, :, : 2 * N_QK].bitcast(I32))
     for quadrant in range(4):
         nc.sync.dma_start(
             out=raw_plane[32 * quadrant : 32 * quadrant + 4, :].bitcast(I32),
             in_=scales_dram[0, 4 * quadrant : 4 * quadrant + 4, :].bitcast(I32),
         )
-    nc.sync.dma_start(out=words[:, 2 * N_QK : 2 * N_QKV].bitcast(I32), in_=words_dram[0, :, 2 * N_QK :].bitcast(I32))
     return raw_words, raw_plane, words, plane
 
 
-def sort_columns(nc, weight):
-    raw_words, raw_plane, words, plane = weight
-    source = raw_words[:].rearrange("p (n i b y) -> p n i b y", n=NORMS, b=2, y=2)
+def sort_words(nc, weight):
+    raw_words, words = weight[0], weight[2]
+    source = raw_words[:, : 2 * N_QK].rearrange("p (n i b y) -> p n i b y", n=NORMS, b=2, y=2)
     target = words[:, : 2 * N_QK].rearrange("p (n b i y) -> p n b i y", n=NORMS, b=2, y=2)
     for b in range(2):
         nc.vector.tensor_copy(out=target[:, :, b], in_=source[:, :, :, b])
+    nc.vector.tensor_copy(out=words[:, 2 * N_QK :].bitcast(I32), in_=raw_words[:, 2 * N_QK :].bitcast(I32))
+
+
+def sort_plane(nc, weight):
+    raw_plane, plane = weight[1], weight[3]
     nc.vector.tensor_copy(
         out=plane[:, :N_QK].rearrange("p (n b i) -> p n b i", n=NORMS, b=2),
         in_=raw_plane[:, :N_QK].rearrange("p (n i b) -> p n b i", n=NORMS, b=2),
     )
-    nc.vector.tensor_copy(out=plane[:, N_QK:N_QKV], in_=raw_plane[:, N_QK:])
+    nc.vector.tensor_copy(out=plane[:, N_QK:].bitcast(I32), in_=raw_plane[:, N_QK:].bitcast(I32))
 
 
 def tile_fluxattention_pa_t_kernel(
@@ -89,6 +93,7 @@ def tile_fluxattention_pa_t_kernel(
         consts = ctx.enter_context(tc.tile_pool(name="consts", bufs=1))
         work = ctx.enter_context(tc.tile_pool(name="work", bufs=3))
         deep = ctx.enter_context(tc.tile_pool(name="deep", bufs=3))
+        terms_pool = ctx.enter_context(tc.tile_pool(name="terms", bufs=4))
         scaled_pool = ctx.enter_context(tc.tile_pool(name="scaled", bufs=5))
         xt_psum = ctx.enter_context(tc.psum_pool(name="xt_psum", bufs=2))
         qk_psum = ctx.enter_context(tc.psum_pool(name="qk_psum", bufs=4))
@@ -102,7 +107,7 @@ def tile_fluxattention_pa_t_kernel(
             if c == 0:
                 sizes = [PAIR, PAIR] + sizes[1:]
             if c == N_CHUNKS - 1:
-                sizes = sizes[1:] + [PAIR, PAIR]
+                sizes = sizes[1:] + [PAIR, 1, 1]
             first = 0
             for size in sizes:
                 groups.append((c, first, size))
@@ -112,9 +117,8 @@ def tile_fluxattention_pa_t_kernel(
         nc.vector.memset(gain_rows[:], 0.0)
         ones = consts.tile([P, P], BF16, name="ones")
         nc.vector.memset(ones[:], 1.0)
-        for s, stream_gains in enumerate(((eqn_scale, ekn_scale), (qn_scale, kn_scale))):
-            for qk, gain in enumerate(stream_gains):
-                nc.scalar.dma_start(out=gain_rows[0:1, s, qk, :], in_=gain.partition_broadcast(1))
+        for qk, gain in enumerate((eqn_scale, ekn_scale)):
+            nc.scalar.dma_start(out=gain_rows[0:1, 0, qk, :], in_=gain.partition_broadcast(1))
 
         x_blocks = []
         table_tiles = []
@@ -137,12 +141,13 @@ def tile_fluxattention_pa_t_kernel(
             )
             table_tiles.append(table)
 
-        load_x(0, 0, PAIR)
+        load_x(0, 0, GROUP)
         weights["txt"] = load_weight(nc, consts, W_eqkv_words, W_eqkv_scales, "txt")
-        load_x(0, PAIR, PAIR)
         load_table(0)
-        load_table(1)
         load_x(0, GROUP, GROUP)
+        load_table(1)
+        for qk, gain in enumerate((qn_scale, kn_scale)):
+            nc.sync.dma_start(out=gain_rows[0:1, 1, qk, :], in_=gain.partition_broadcast(1))
         for c in range(1, N_CHUNKS):
             for first in range(0, T, GROUP):
                 load_x(c, first, GROUP)
@@ -165,16 +170,17 @@ def tile_fluxattention_pa_t_kernel(
         def transpose(g):
             c, first, size = groups[g]
             grouped = work.tile([P, GROUP, P, 4], BF16, name="grouped", align_bytes=64)
-            for pair in range(size // PAIR):
+            for start in range(0, size, PAIR):
+                blocks = min(PAIR, size - start)
                 xt = xt_psum.tile([P, PAIR, 2, P], F32, name="xt")
-                for j in range(PAIR):
-                    x_sb, place = x_blocks[c * T + first + PAIR * pair + j]
+                for j in range(blocks):
+                    x_sb, place = x_blocks[c * T + first + start + j]
                     x_words = x_sb[:, place, :].bitcast(F32)
                     for u in range(2):
                         nc.tensor.transpose(xt[:, j, u, :], x_words[:, u : DM // 2 : 2], ident[:])
                 nc.scalar.copy(
-                    out=grouped[:, PAIR * pair : PAIR * (pair + 1), :, :].bitcast(F32),
-                    in_=xt[:].rearrange("p j u r -> p j r u"),
+                    out=grouped[:, start : start + blocks, :, :].bitcast(F32),
+                    in_=xt[:, :blocks].rearrange("p j u r -> p j r u"),
                 )
             state["grouped", g] = grouped
 
@@ -229,11 +235,11 @@ def tile_fluxattention_pa_t_kernel(
                 )
 
             qk_tiles = []
-            for pair in range(size // PAIR):
+            for start in range(0, size, PAIR):
                 qk_ps = qk_psum.tile([P, PAIR, N_QK], F32, name="qk_ps")
                 qk_tiles.append(qk_ps)
-                for j in range(PAIR):
-                    one_pass(qk_ps[:, j, :], PAIR * pair + j, slice(0, N_QK))
+                for j in range(min(PAIR, size - start)):
+                    one_pass(qk_ps[:, j, :], start + j, slice(0, N_QK))
             v_ps = v_psum.tile([P, GROUP, HD], F32, name="v_ps")
             for j in range(size):
                 one_pass(v_ps[:, j, :], j, slice(N_QK, N_QKV))
@@ -278,7 +284,7 @@ def tile_fluxattention_pa_t_kernel(
             qk_tiles = state["y", g][0]
             inv_rms = state["inv_rms", g]
             scaled = state["scaled", c]
-            terms = work.tile([P, 2, GROUP, HEADS, 2 * D], F32, name="terms")
+            terms = terms_pool.tile([P, 2, GROUP, HEADS, 2 * D], F32, name="terms")
             for j in range(size):
                 for n in range(NORMS):
                     qk, head = divmod(n, HEADS)
@@ -299,7 +305,7 @@ def tile_fluxattention_pa_t_kernel(
             if first == 0:
                 state["rotated", c] = deep.tile([P, 2, T, HD], F32, name="rotated")
             rotated = state["rotated", c]
-            if g == len(groups) - 1:
+            if size < PAIR:
                 engine, parts = nc.vector, (slice(0, 1), slice(1, 2))
             else:
                 engine, parts = nc.gpsimd, (slice(0, 2),)
@@ -315,6 +321,8 @@ def tile_fluxattention_pa_t_kernel(
                     store((out_0, out_1)[qk], rotated[:, qk], g)
 
         jobs = [(c, half, qk) for c in range(N_CHUNKS) for half in range(2) for qk in range(2)]
+        vector_head = jobs[:HEAD_JOBS_VECTOR]
+        gpsimd_head = jobs[HEAD_JOBS_VECTOR : HEAD_JOBS_VECTOR + HEAD_JOBS_GPSIMD]
         later_jobs = jobs[HEAD_JOBS_VECTOR + HEAD_JOBS_GPSIMD :]
         first_turn = 3
         turns = len(groups) - first_turn - 2
@@ -326,9 +334,7 @@ def tile_fluxattention_pa_t_kernel(
             numbers = range(turn * len(later_jobs) // turns, (turn + 1) * len(later_jobs) // turns)
             return [later_jobs[n] for n in numbers if (n % GPSIMD_TURN == GPSIMD_TURN - 1) == gpsimd]
 
-        sort_columns(nc, weights["txt"])
-        transpose(0)
-        for s in range(2):
+        def spread_gains(s):
             for qk in range(2):
                 nc.tensor.matmul(
                     out=gains_ps[:, s, qk, :],
@@ -337,6 +343,10 @@ def tile_fluxattention_pa_t_kernel(
                     start=True,
                     stop=True,
                 )
+            nc.vector.tensor_copy(out=gains_sb[:, s], in_=gains_ps[:, s])
+
+        sort_words(nc, weights["txt"])
+        transpose(0)
         for step in range(len(groups) + 3):
             if step + 1 < len(groups) and step != 1:
                 transpose(step + 1)
@@ -350,13 +360,19 @@ def tile_fluxattention_pa_t_kernel(
             if step < len(groups):
                 quantise(step)
             if step == 0:
-                nc.vector.tensor_copy(out=gains_sb[:], in_=gains_ps[:])
-                for job in jobs[:HEAD_JOBS_VECTOR]:
+                sort_plane(nc, weights["txt"])
+                spread_gains(0)
+            if step == 1:
+                spread_gains(1)
+            if step < 2:
+                for job in vector_head[2 * step : 2 * (step + 1)]:
                     scale_table(nc.vector, gains_ps, job)
-                for job in jobs[HEAD_JOBS_VECTOR : HEAD_JOBS_VECTOR + HEAD_JOBS_GPSIMD]:
-                    scale_table(nc.gpsimd, gains_sb, job)
+                for job in gpsimd_head:
+                    if int(job[0] >= TXT_CHUNKS) == step:
+                        scale_table(nc.gpsimd, gains_sb, job)
             if step == first_turn:
-                sort_columns(nc, weights["img"])
+                sort_words(nc, weights["img"])
+                sort_plane(nc, weights["img"])
             for job in turn_jobs(step, False):
                 scale_table(nc.vector, gains_ps, job)
             if step >= 3:

from contextlib import ExitStack

import concourse.mybir as mybir
from concourse.masks import make_identity

F32 = mybir.dt.float32
BF16 = mybir.dt.bfloat16
I32 = mybir.dt.int32
U32 = mybir.dt.uint32
U8 = mybir.dt.uint8
FP8X4 = mybir.dt.float8_e4m3fn_x4
FP4X4 = mybir.dt.float4_e2m1fn_x4
ACT = mybir.ActivationFunctionType
ALU = mybir.AluOpType

P = 128
DM = 512
L_TXT = 2048
L_IMG = 6144
HEADS = 2
D = 64
HD = HEADS * D
N_QK = 2 * HD
N_QKV = 3 * HD
EPS = 1e-6

T = 8
CHUNK = P * T
N_CHUNKS = (L_TXT + L_IMG) // CHUNK
TXT_CHUNKS = L_TXT // CHUNK
PAIR = 2
GROUP = 4
HEAD_JOBS_VECTOR = 4
HEAD_JOBS_GPSIMD = 6
GPSIMD_TURN = 3
NORMS = 2 * HEADS

FLOPS = 2 * (L_TXT + L_IMG) * DM * N_QKV


def load_weight(nc, consts, words_dram, scales_dram, label):
    raw_words = consts.tile([P, 2 * N_QKV], U8, name=label + "_raw_words", align_bytes=64)
    words = consts.tile([P, 2 * N_QKV], U8, name=label + "_words", align_bytes=64)
    raw_plane = consts.tile([P, N_QKV], U8, name=label + "_raw_plane", align_bytes=64)
    plane = consts.tile([P, N_QKV], U8, name=label + "_plane", align_bytes=64)
    nc.sync.dma_start(out=raw_words[:].bitcast(I32), in_=words_dram[0].bitcast(I32))
    nc.vector.memset(raw_plane[:].bitcast(I32), 0)
    for quadrant in range(4):
        nc.sync.dma_start(
            out=raw_plane[32 * quadrant : 32 * quadrant + 4, :].bitcast(I32),
            in_=scales_dram[0, 4 * quadrant : 4 * quadrant + 4, :].bitcast(I32),
        )
    return raw_words, raw_plane, words, plane


def sort_words(nc, weight):
    raw_words, words = weight[0], weight[2]
    source = raw_words[:, : 2 * N_QK].rearrange("p (n i b y) -> p n i b y", n=NORMS, b=2, y=2)
    target = words[:, : 2 * N_QK].rearrange("p (n b i y) -> p n b i y", n=NORMS, b=2, y=2)
    for b in range(2):
        nc.vector.tensor_copy(out=target[:, :, b], in_=source[:, :, :, b])
    nc.vector.tensor_copy(out=words[:, 2 * N_QK :].bitcast(I32), in_=raw_words[:, 2 * N_QK :].bitcast(I32))


def sort_plane(nc, weight):
    raw_plane, plane = weight[1], weight[3]
    nc.vector.tensor_copy(
        out=plane[:, :N_QK].rearrange("p (n b i) -> p n b i", n=NORMS, b=2),
        in_=raw_plane[:, :N_QK].rearrange("p (n i b) -> p n b i", n=NORMS, b=2),
    )
    nc.vector.tensor_copy(out=plane[:, N_QK:].bitcast(I32), in_=raw_plane[:, N_QK:].bitcast(I32))


def tile_fluxattention_pa_t_kernel(
    tc,
    hidden_states,
    encoder_hidden_states,
    image_rotary_emb,
    W_iqkv_words,
    W_iqkv_scales,
    W_eqkv_words,
    W_eqkv_scales,
    qn_scale,
    kn_scale,
    eqn_scale,
    ekn_scale,
    out_0,
    out_1,
    out_2,
):
    nc = tc.nc
    with ExitStack() as ctx:
        consts = ctx.enter_context(tc.tile_pool(name="consts", bufs=1))
        work = ctx.enter_context(tc.tile_pool(name="work", bufs=3))
        deep = ctx.enter_context(tc.tile_pool(name="deep", bufs=3))
        terms_pool = ctx.enter_context(tc.tile_pool(name="terms", bufs=4))
        scaled_pool = ctx.enter_context(tc.tile_pool(name="scaled", bufs=5))
        xt_psum = ctx.enter_context(tc.psum_pool(name="xt_psum", bufs=2))
        qk_psum = ctx.enter_context(tc.psum_pool(name="qk_psum", bufs=4))
        v_psum = ctx.enter_context(tc.psum_pool(name="v_psum", bufs=1))
        gain_psum = ctx.enter_context(tc.psum_pool(name="gain_psum", bufs=1))
        ctx.enter_context(tc.manual_schedule())

        groups = []
        for c in range(N_CHUNKS):
            sizes = [GROUP] * (T // GROUP)
            if c == 0:
                sizes = [PAIR, PAIR] + sizes[1:]
            if c == N_CHUNKS - 1:
                sizes = sizes[1:] + [PAIR, 1, 1]
            first = 0
            for size in sizes:
                groups.append((c, first, size))
                first += size

        gain_rows = consts.tile([P, 2, 2, D], BF16, name="gain_rows")
        nc.vector.memset(gain_rows[:], 0.0)
        ones = consts.tile([P, P], BF16, name="ones")
        nc.vector.memset(ones[:], 1.0)
        for qk, gain in enumerate((eqn_scale, ekn_scale)):
            nc.scalar.dma_start(out=gain_rows[0:1, 0, qk, :], in_=gain.partition_broadcast(1))

        x_blocks = []
        table_tiles = []
        weights = {}

        def load_x(c, first, size):
            if c < TXT_CHUNKS:
                rows = encoder_hidden_states[0, c * CHUNK : (c + 1) * CHUNK, :]
            else:
                rows = hidden_states[0, (c - TXT_CHUNKS) * CHUNK : (c - TXT_CHUNKS + 1) * CHUNK, :]
            x_sb = consts.tile([P, size, DM], BF16, name="x_%d_%d" % (c, first))
            nc.sync.dma_start(out=x_sb[:], in_=rows.rearrange("(p t) k -> p t k", t=T)[:, first : first + size, :])
            x_blocks.extend((x_sb, j) for j in range(size))

        def load_table(c):
            table = consts.tile([P, T, 2 * D], BF16, name="table_%d" % c)
            nc.sync.dma_start(
                out=table[:],
                in_=image_rotary_emb[c * CHUNK : (c + 1) * CHUNK].rearrange("(p t) i f -> p t (i f)", t=T),
            )
            table_tiles.append(table)

        load_x(0, 0, GROUP)
        weights["txt"] = load_weight(nc, consts, W_eqkv_words, W_eqkv_scales, "txt")
        load_table(0)
        load_x(0, GROUP, GROUP)
        load_table(1)
        for qk, gain in enumerate((qn_scale, kn_scale)):
            nc.sync.dma_start(out=gain_rows[0:1, 1, qk, :], in_=gain.partition_broadcast(1))
        for c in range(1, N_CHUNKS):
            for first in range(0, T, GROUP):
                load_x(c, first, GROUP)
            if c + 1 < N_CHUNKS:
                load_table(c + 1)
            if c == 1:
                weights["img"] = load_weight(nc, consts, W_iqkv_words, W_iqkv_scales, "img")

        ident = consts.tile([P, P], F32, name="ident")
        make_identity(nc, ident[:])
        gains_ps = gain_psum.tile([P, 2, 2, D], F32, name="gains_ps")
        gains_sb = consts.tile([P, 2, 2, D], F32, name="gains_sb")
        eps = consts.tile([P, 1], F32, name="eps")
        nc.vector.memset(eps[:], EPS)
        first_root = consts.tile([P, 1], F32, name="first_root")
        nc.scalar.activation(out=first_root[:], in_=eps[:], func=ACT.Abs_reciprocal_sqrt, bias=eps[:], scale=1.0 / D)

        state = {}

        def transpose(g):
            c, first, size = groups[g]
            grouped = work.tile([P, GROUP, P, 4], BF16, name="grouped", align_bytes=64)
            for start in range(0, size, PAIR):
                blocks = min(PAIR, size - start)
                xt = xt_psum.tile([P, PAIR, 2, P], F32, name="xt")
                for j in range(blocks):
                    x_sb, place = x_blocks[c * T + first + start + j]
                    x_words = x_sb[:, place, :].bitcast(F32)
                    for u in range(2):
                        nc.tensor.transpose(xt[:, j, u, :], x_words[:, u : DM // 2 : 2], ident[:])
                nc.scalar.copy(
                    out=grouped[:, start : start + blocks, :, :].bitcast(F32),
                    in_=xt[:, :blocks].rearrange("p j u r -> p j r u"),
                )
            state["grouped", g] = grouped

        def quantise(g):
            size = groups[g][2]
            codes = work.tile([P, GROUP * P], U32, name="codes", align_bytes=64)
            x_plane = work.tile([P, GROUP * P], U8, name="x_plane", align_bytes=64)
            nc.vector.quantize_mx(
                out=codes[:, : size * P].bitcast(FP8X4),
                scales=x_plane[:, : size * P],
                in_=state["grouped", g][:, :size].rearrange("p j r t -> p (j r t)"),
            )
            state["codes", g] = codes, x_plane

        def scale_table(engine, gains, job):
            c, half, qk = job
            if ("scaled", c) not in state:
                state["scaled", c] = scaled_pool.tile([P, T, 2, 2 * D], F32, name="scaled")
            tokens = slice(half * (T // 2), (half + 1) * (T // 2))
            engine.tensor_tensor(
                out=state["scaled", c][:, tokens, qk, :].rearrange("p t (b i a) -> p t b i a", b=2, a=2),
                in0=gains[:, int(c >= TXT_CHUNKS), qk, :]
                .rearrange("p (o b i z) -> p o b i z", o=1, b=2, z=1)
                .to_broadcast([P, T // 2, 2, D // 2, 2]),
                in1=table_tiles[c][:, tokens, :].rearrange("p t (i a b) -> p t b i a", a=2, b=2),
                op=ALU.mult,
            )

        def store(out, tile, g):
            c, first, size = groups[g]
            rows = out[0, c * CHUNK : (c + 1) * CHUNK, :].rearrange("(p t) f -> p t f", t=T)
            if c == N_CHUNKS - 1:
                blocks = slice(first, first + size)
                nc.sync.dma_start(out=rows[:, blocks, :], in_=tile[:, blocks, :])
            elif first + size == T:
                nc.sync.dma_start(out=rows, in_=tile[:])

        def project(g):
            c, first, size = groups[g]
            codes, x_plane = state["codes", g]
            w_words, w_plane = weights["txt" if c < TXT_CHUNKS else "img"][2:]

            def one_pass(out, j, columns):
                nc.tensor.matmul_mx(
                    out=out,
                    lhsT=codes[:, j * P : (j + 1) * P].bitcast(FP8X4),
                    lhsT_scale=x_plane[:, j * P : (j + 1) * P],
                    rhs=w_words[:, 2 * columns.start : 2 * columns.stop].bitcast(FP4X4),
                    rhs_scale=w_plane[:, columns],
                    start=True,
                    stop=True,
                )

            qk_tiles = []
            for start in range(0, size, PAIR):
                qk_ps = qk_psum.tile([P, PAIR, N_QK], F32, name="qk_ps")
                qk_tiles.append(qk_ps)
                for j in range(min(PAIR, size - start)):
                    one_pass(qk_ps[:, j, :], start + j, slice(0, N_QK))
            v_ps = v_psum.tile([P, GROUP, HD], F32, name="v_ps")
            for j in range(size):
                one_pass(v_ps[:, j, :], j, slice(N_QK, N_QKV))
            state["y", g] = qk_tiles, v_ps

        def square(g):
            c, first, size = groups[g]
            qk_tiles = state["y", g][0]
            squares = work.tile([P, NORMS, D], BF16, name="squares")
            sums = deep.tile([P, GROUP * NORMS], F32, name="sums")
            for j in range(size):
                for n in range(NORMS):
                    nc.scalar.activation(
                        out=squares[:, n, :],
                        in_=qk_tiles[j // PAIR][:, j % PAIR, n * D : (n + 1) * D],
                        func=ACT.Square,
                        accum_out=sums[:, j * NORMS + n : j * NORMS + n + 1],
                    )
            state["sums", g] = sums

        def finish_norms(g):
            c, first, size = groups[g]
            v_ps = state["y", g][1]
            sums = state["sums", g]
            if first == 0:
                state["v_sb", c] = deep.tile([P, T, HD], F32, name="v_sb")
            v_sb = state["v_sb", c]
            nc.scalar.copy(out=v_sb[:, first : first + size, :], in_=v_ps[:, :size, :])
            store(out_2, v_sb, g)
            inv_rms = deep.tile([P, GROUP * NORMS], F32, name="inv_rms")
            nc.scalar.activation(
                out=inv_rms[:, : size * NORMS],
                in_=sums[:, : size * NORMS],
                func=ACT.Abs_reciprocal_sqrt,
                bias=eps[:],
                scale=1.0 / D,
            )
            state["inv_rms", g] = inv_rms

        def multiply(g):
            c, first, size = groups[g]
            qk_tiles = state["y", g][0]
            inv_rms = state["inv_rms", g]
            scaled = state["scaled", c]
            terms = terms_pool.tile([P, 2, GROUP, HEADS, 2 * D], F32, name="terms")
            for j in range(size):
                for n in range(NORMS):
                    qk, head = divmod(n, HEADS)
                    y = qk_tiles[j // PAIR][:, j % PAIR, n * D : (n + 1) * D].rearrange("p (f o) -> p f o", o=1)
                    nc.vector.scalar_tensor_tensor(
                        out=terms[:, qk, j, head].rearrange("p (f a) -> p f a", a=2),
                        in0=y.to_broadcast([P, D, 2]),
                        scalar=inv_rms[:, j * NORMS + n : j * NORMS + n + 1],
                        in1=scaled[:, first + j, qk].rearrange("p (f a) -> p f a", a=2),
                        op0=ALU.mult,
                        op1=ALU.mult,
                    )
            state["terms", g] = terms

        def add_terms(g):
            c, first, size = groups[g]
            terms = state["terms", g]
            if first == 0:
                state["rotated", c] = deep.tile([P, 2, T, HD], F32, name="rotated")
            rotated = state["rotated", c]
            if size < PAIR:
                engine, parts = nc.vector, (slice(0, 1), slice(1, 2))
            else:
                engine, parts = nc.gpsimd, (slice(0, 2),)
            for part in parts:
                both = terms[:, part, :size].rearrange("p q j h (b f) -> p q (j h) b f", b=2)
                engine.tensor_tensor(
                    out=rotated[:, part, first : first + size, :].rearrange("p q j (h f) -> p q (j h) f", h=HEADS),
                    in0=both[:, :, :, 0],
                    in1=both[:, :, :, 1],
                    op=ALU.add,
                )
                for qk in range(part.start, part.stop):
                    store((out_0, out_1)[qk], rotated[:, qk], g)

        jobs = [(c, half, qk) for c in range(N_CHUNKS) for half in range(2) for qk in range(2)]
        vector_head = jobs[:HEAD_JOBS_VECTOR]
        gpsimd_head = jobs[HEAD_JOBS_VECTOR : HEAD_JOBS_VECTOR + HEAD_JOBS_GPSIMD]
        later_jobs = jobs[HEAD_JOBS_VECTOR + HEAD_JOBS_GPSIMD :]
        first_turn = 3
        turns = len(groups) - first_turn - 2

        def turn_jobs(step, gpsimd):
            turn = step - first_turn
            if not 0 <= turn < turns:
                return []
            numbers = range(turn * len(later_jobs) // turns, (turn + 1) * len(later_jobs) // turns)
            return [later_jobs[n] for n in numbers if (n % GPSIMD_TURN == GPSIMD_TURN - 1) == gpsimd]

        def spread_gains(s):
            for qk in range(2):
                nc.tensor.matmul(
                    out=gains_ps[:, s, qk, :],
                    lhsT=ones[:],
                    rhs=gain_rows[:, s, qk, :].rearrange("p (i b) -> p b i", b=2),
                    start=True,
                    stop=True,
                )
            nc.vector.tensor_copy(out=gains_sb[:, s], in_=gains_ps[:, s])

        sort_words(nc, weights["txt"])
        transpose(0)
        for step in range(len(groups) + 3):
            if step + 1 < len(groups) and step != 1:
                transpose(step + 1)
            if 1 <= step < len(groups) + 1:
                project(step - 1)
                square(step - 1)
            if step == 1:
                transpose(step + 1)
            if 1 <= step < len(groups) + 1:
                finish_norms(step - 1)
            if step < len(groups):
                quantise(step)
            if step == 0:
                sort_plane(nc, weights["txt"])
                spread_gains(0)
            if step == 1:
                spread_gains(1)
            if step < 2:
                for job in vector_head[2 * step : 2 * (step + 1)]:
                    scale_table(nc.vector, gains_ps, job)
                for job in gpsimd_head:
                    if int(job[0] >= TXT_CHUNKS) == step:
                        scale_table(nc.gpsimd, gains_sb, job)
            if step == first_turn:
                sort_words(nc, weights["img"])
                sort_plane(nc, weights["img"])
            for job in turn_jobs(step, False):
                scale_table(nc.vector, gains_ps, job)
            if step >= 3:
                add_terms(step - 3)
            for job in turn_jobs(step, True):
                scale_table(nc.gpsimd, gains_sb, job)
            if 2 <= step < len(groups) + 2:
                multiply(step - 2)
